import numpy as np
import ml_dtypes


def mxq(x, axis, fmt="e4m3"):
    dtype, down = {"e4m3": (ml_dtypes.float8_e4m3fn, 7), "e5m2": (ml_dtypes.float8_e5m2, 14)}[fmt]
    v = np.moveaxis(np.asarray(x, np.float32).astype(ml_dtypes.bfloat16).astype(np.float64), axis, -1)
    blocks = v.reshape(v.shape[:-1] + (-1, 32))
    amax = np.abs(blocks).max(-1, keepdims=True)
    byte = np.maximum(np.where(amax > 0, np.frexp(amax)[1] - 1 + 127, 0) - down, 1)
    scale = np.exp2(byte - 127.0)
    codes = (blocks / scale).astype(np.float32).astype(dtype).astype(np.float64)
    return np.moveaxis((codes * scale).reshape(v.shape), -1, axis)


WIDE = False


def mx_kscale(k):
    if not WIDE:
        return np.ones(k)
    levels = np.array([10, -10, 5, -5, 0])
    a = np.random.permutation(np.resize(levels, k // 512 * 4)).reshape(k // 512, 4)
    idx = np.arange(k)
    return np.exp2(a[idx // 512, idx % 128 // 32])


BF16 = ml_dtypes.bfloat16


def bf(x):
    return np.asarray(x, np.float32).astype(BF16)


def f64(x):
    return np.asarray(x).astype(np.float64)


B, S, D, H, HKV, DH, QB = 1, 512, 2048, 16, 4, 128, 512
THETA = 1000000.0


def rotate_half(u):
    return np.stack((-u[..., 1::2], u[..., ::2]), axis=-1).reshape(u.shape)


def setup_inputs():
    s = mx_kscale(D)
    inv_freq = 1.0 / THETA ** (np.arange(0, DH, 2) / DH)
    emb = np.repeat(np.outer(np.arange(S), inv_freq), 2, axis=-1)
    return {"x": bf(np.random.standard_normal((B, S, D)) * s),
            "cos": bf(np.cos(emb)),
            "sin": bf(np.sin(emb)),
            "Wq": bf(np.random.standard_normal((D, H * DH)) * 1.5 / np.sqrt(D) / s[:, None]),
            "Wk": bf(np.random.standard_normal((D, HKV * DH)) * 1.5 / np.sqrt(D) / s[:, None]),
            "Wv": bf(np.random.standard_normal((D, HKV * DH)) / np.sqrt(D) / s[:, None])}


def reference(x, cos, sin, Wq, Wk, Wv):
    xq = mxq(f64(x), 2, "e4m3")
    q = (xq @ mxq(f64(Wq), 0, "e4m3")).reshape(B, S, H, DH).transpose(0, 2, 1, 3)
    k = (xq @ mxq(f64(Wk), 0, "e4m3")).reshape(B, S, HKV, DH).transpose(0, 2, 1, 3)
    v = (xq @ mxq(f64(Wv), 0, "e4m3")).reshape(B, S, HKV, DH).transpose(0, 2, 1, 3)
    c = f64(cos)[None, None, :, :]
    sn = f64(sin)[None, None, :, :]
    q = q * c + rotate_half(q) * sn
    k = k * c + rotate_half(k) * sn
    return q, k, v

@@ -1,0 +1,197 @@
+from contextlib import ExitStack
+
+import concourse.mybir as mybir
+from concourse.masks import make_identity
+
+F32 = mybir.dt.float32
+BF16 = mybir.dt.bfloat16
+U32 = mybir.dt.uint32
+U8 = mybir.dt.uint8
+FP8X4 = mybir.dt.float8_e4m3fn_x4
+MULT = mybir.AluOpType.mult
+ADD = mybir.AluOpType.add
+
+P = 128
+PACK = 4
+K_PASS = P * PACK
+S = 512
+D = 2048
+DH = 128
+PAIRS = DH // 2
+S_TILES = S // P
+PASSES = D // K_PASS
+CHUNK = 512
+HEADS = CHUNK // DH
+AHEAD = 2
+VECTOR_COLS = 128
+
+FLOPS = 2 * S * D * (2048 + 512 + 512)
+
+
+def tile_attention_pa_kernel(tc, x, cos, sin, Wq, Wk, Wv, out_0, out_1, out_2):
+    nc = tc.nc
+    with ExitStack() as ctx:
+        consts = ctx.enter_context(tc.tile_pool(name="consts", bufs=1))
+        raw_pool = ctx.enter_context(tc.tile_pool(name="raw", bufs=1))
+        x_group_pool = ctx.enter_context(tc.tile_pool(name="x_group", bufs=2))
+        w_group_pool = ctx.enter_context(tc.tile_pool(name="w_group", bufs=4))
+        w_code_pool = ctx.enter_context(tc.tile_pool(name="w_code", bufs=AHEAD + 1))
+        cross_pool = ctx.enter_context(tc.tile_pool(name="cross", bufs=4))
+        result_pool = ctx.enter_context(tc.tile_pool(name="result", bufs=3))
+        psum = ctx.enter_context(tc.psum_pool(name="psum", bufs=8))
+
+        x_rows = x.rearrange("b (p t) k -> t p (b k)", t=S_TILES)
+        x_sb = []
+        for t in range(S_TILES):
+            x_t = raw_pool.tile([P, D], BF16, name="x_rows_%d" % t)
+            nc.sync.dma_start(out=x_t[:], in_=x_rows[t])
+            x_sb.append(x_t)
+
+        def load_chunk(w, first_col, label):
+            by_pass = w.rearrange("(g p j) n -> g p j n", p=P, j=PACK)
+            tiles = []
+            for g in range(PASSES):
+                raw = raw_pool.tile([P, PACK, CHUNK], BF16, name="%s_pass%d" % (label, g))
+                nc.sync.dma_start(out=raw[:], in_=by_pass[g, :, :, first_col : first_col + CHUNK])
+                tiles.append(raw)
+            return tiles
+
+        q_out = out_0.rearrange("b h (p t) d -> p (b h) (t d)", t=S_TILES)
+        k_out = out_1.rearrange("b h (p t) d -> p (b h) (t d)", t=S_TILES)
+        v_out = out_2.rearrange("b h (p t) d -> p (b h) (t d)", t=S_TILES)
+
+        chunks = []
+        chunks.append((load_chunk(Wk, 0, "wk"), k_out, True))
+        cos_sb = consts.tile([P, S_TILES, DH], BF16)
+        sin_sb = consts.tile([P, S_TILES, DH], BF16)
+        nc.sync.dma_start(out=cos_sb[:].rearrange("p t d -> p (t d)"), in_=cos.rearrange("(p t) d -> p (t d)", t=S_TILES))
+        nc.sync.dma_start(out=sin_sb[:].rearrange("p t d -> p (t d)"), in_=sin.rearrange("(p t) d -> p (t d)", t=S_TILES))
+        for n in range(2048 // CHUNK):
+            chunks.append((load_chunk(Wq, n * CHUNK, "wq%d" % n), q_out[:, n * HEADS : (n + 1) * HEADS, :], True))
+        chunks.append((load_chunk(Wv, 0, "wv"), v_out, False))
+
+        sin_pairs = sin_sb[:].rearrange("p t (i e) -> p t i e", e=2)
+        neg_sin_even = consts.tile([P, S_TILES, PAIRS], F32)
+        sin_odd = consts.tile([P, S_TILES, PAIRS], F32)
+        nc.vector.tensor_scalar_mul(out=neg_sin_even[:], in0=sin_pairs[:, :, :, 0], scalar1=-1.0)
+        nc.vector.tensor_copy(out=sin_odd[:], in_=sin_pairs[:, :, :, 1])
+
+        ident = consts.tile([P, P], F32)
+        make_identity(nc, ident[:])
+        x_codes = []
+        x_scales = []
+        for t in range(S_TILES):
+            words = x_sb[t][:].bitcast(F32).rearrange("s (g w u) -> s g u w", g=PASSES, u=2)
+            grouped_x = x_group_pool.tile([P, PASSES, P, PACK], BF16, align_bytes=64)
+            grouped_words = grouped_x[:].bitcast(F32)
+            for half in range(2):
+                turned = psum.tile([P, 2, 2, P], F32, tag="bank")
+                for g2 in range(2):
+                    for u in range(2):
+                        nc.tensor.transpose(turned[:, g2, u, :], words[:, 2 * half + g2, u, :], ident[:])
+                if half == 0:
+                    nc.vector.tensor_copy(out=grouped_words[:, 0:2, :, :], in_=turned[:].rearrange("p g u s -> p g s u"))
+                else:
+                    nc.scalar.copy(out=grouped_words[:, 2:4, :, :], in_=turned[:].rearrange("p g u s -> p g s u"))
+            codes_t = consts.tile([P, PASSES * P], U32, name="x_codes_%d" % t, align_bytes=64)
+            scales_t = consts.tile([P, PASSES * P], U8, name="x_scales_%d" % t, align_bytes=64)
+            nc.vector.quantize_mx(
+                out=codes_t[:].bitcast(FP8X4),
+                scales=scales_t[:],
+                in_=grouped_x[:].rearrange("p g s j -> p (g s j)"),
+            )
+            x_codes.append(codes_t)
+            x_scales.append(scales_t)
+
+        w_codes = {}
+        w_scales = {}
+        w_grouped = {}
+
+        def regroup(c, g):
+            if g == 0:
+                w_codes[c] = w_code_pool.tile([P, PASSES, CHUNK], U32, name="w_codes", align_bytes=64)
+                w_scales[c] = w_code_pool.tile([P, PASSES, CHUNK], U8, name="w_scales", align_bytes=64)
+            raw = chunks[c][0][g]
+            grouped = w_group_pool.tile([P, CHUNK, PACK], BF16, name="w_grouped", align_bytes=64)
+            split = CHUNK - VECTOR_COLS
+            nc.scalar.copy(
+                out=grouped[:, 0:split, :].rearrange("p (c i) j -> p c j i", i=4),
+                in_=raw[:, :, 0:split].rearrange("p j (c i) -> p c j i", i=4),
+            )
+            nc.vector.tensor_copy(
+                out=grouped[:, split:CHUNK, :].rearrange("p (c i) j -> p c j i", i=4),
+                in_=raw[:, :, split:CHUNK].rearrange("p j (c i) -> p c j i", i=4),
+            )
+            w_grouped[(c, g)] = grouped
+
+        def quantise(c, g):
+            nc.vector.quantize_mx(
+                out=w_codes[c][:, g, :].bitcast(FP8X4),
+                scales=w_scales[c][:, g, :],
+                in_=w_grouped[(c, g)][:].rearrange("p w j -> p (w j)"),
+            )
+
+        def multiply(c):
+            banks = []
+            for t in range(S_TILES):
+                acc = psum.tile([P, CHUNK], F32, tag="bank")
+                for g in range(PASSES):
+                    nc.tensor.matmul_mx(
+                        out=acc[:],
+                        lhsT=x_codes[t][:, g * P : (g + 1) * P].bitcast(FP8X4),
+                        lhsT_scale=x_scales[t][:, g * P : (g + 1) * P],
+                        rhs=w_codes[c][:, g, :].bitcast(FP8X4),
+                        rhs_scale=w_scales[c][:, g, :],
+                        start=(g == 0),
+                        stop=(g == PASSES - 1),
+                    )
+                banks.append(acc)
+            return banks
+
+        def rotate(acc, t, result):
+            straight = result[:, :, t, :]
+            nc.vector.tensor_tensor(
+                out=straight,
+                in0=acc[:].rearrange("p (h d) -> p h d", h=HEADS),
+                in1=cos_sb[:, t, :].unsqueeze(1).to_broadcast([P, HEADS, DH]),
+                op=MULT,
+            )
+            pairs = acc[:].rearrange("p (h i e) -> p h i e", h=HEADS, e=2)
+            cross = cross_pool.tile([P, 2, HEADS, PAIRS], F32)
+            nc.vector.tensor_tensor(
+                out=cross[:, 0, :, :],
+                in0=pairs[:, :, :, 1],
+                in1=neg_sin_even[:, t, :].unsqueeze(1).to_broadcast([P, HEADS, PAIRS]),
+                op=MULT,
+            )
+            nc.vector.tensor_tensor(
+                out=cross[:, 1, :, :],
+                in0=pairs[:, :, :, 0],
+                in1=sin_odd[:, t, :].unsqueeze(1).to_broadcast([P, HEADS, PAIRS]),
+                op=MULT,
+            )
+            nc.gpsimd.tensor_tensor(
+                out=straight.rearrange("p h (i e) -> p h i e", e=2),
+                in0=straight.rearrange("p h (i e) -> p h i e", e=2),
+                in1=cross[:].rearrange("p e h i -> p h i e"),
+                op=ADD,
+            )
+
+        for c in range(AHEAD):
+            for g in range(PASSES):
+                regroup(c, g)
+                quantise(c, g)
+
+        for c in range(len(chunks)):
+            banks = multiply(c)
+            result = result_pool.tile([P, HEADS, S_TILES, DH], F32)
+            for t in range(S_TILES):
+                if c + AHEAD < len(chunks):
+                    regroup(c + AHEAD, t)
+                if chunks[c][2]:
+                    rotate(banks[t], t, result)
+                else:
+                    nc.scalar.copy(out=result[:, :, t, :], in_=banks[t][:].rearrange("p (h d) -> p h d", h=HEADS))
+                if c + AHEAD < len(chunks):
+                    quantise(c + AHEAD, t)
+            nc.gpsimd.dma_start(out=chunks[c][1], in_=result[:].rearrange("p h t d -> p h (t d)"))

@@ -22,8 +22,8 @@ S_TILES = S // P
 PASSES = D // K_PASS
 CHUNK = 512
 HEADS = CHUNK // DH
-AHEAD = 2
-VECTOR_COLS = 128
+RAW_CHUNKS = 4
+VECTOR_COLS = 96
 
 FLOPS = 2 * S * D * (2048 + 512 + 512)
 
@@ -32,57 +32,144 @@ def tile_attention_pa_kernel(tc, x, cos, sin, Wq, Wk, Wv, out_0, out_1, out_2):
     nc = tc.nc
     with ExitStack() as ctx:
         consts = ctx.enter_context(tc.tile_pool(name="consts", bufs=1))
-        raw_pool = ctx.enter_context(tc.tile_pool(name="raw", bufs=1))
+        x_pool = ctx.enter_context(tc.tile_pool(name="x_rows", bufs=S_TILES))
+        raw_pool = ctx.enter_context(tc.tile_pool(name="raw", bufs=RAW_CHUNKS * PASSES))
         x_group_pool = ctx.enter_context(tc.tile_pool(name="x_group", bufs=2))
-        w_group_pool = ctx.enter_context(tc.tile_pool(name="w_group", bufs=4))
-        w_code_pool = ctx.enter_context(tc.tile_pool(name="w_code", bufs=AHEAD + 1))
+        w_group_pool = ctx.enter_context(tc.tile_pool(name="w_group", bufs=2 * PASSES))
+        w_code_pool = ctx.enter_context(tc.tile_pool(name="w_code", bufs=2))
         cross_pool = ctx.enter_context(tc.tile_pool(name="cross", bufs=4))
-        result_pool = ctx.enter_context(tc.tile_pool(name="result", bufs=3))
+        result_pool = ctx.enter_context(tc.tile_pool(name="result", bufs=4))
         psum = ctx.enter_context(tc.psum_pool(name="psum", bufs=8))
-
-        x_rows = x.rearrange("b (p t) k -> t p (b k)", t=S_TILES)
-        x_sb = []
-        for t in range(S_TILES):
-            x_t = raw_pool.tile([P, D], BF16, name="x_rows_%d" % t)
-            nc.sync.dma_start(out=x_t[:], in_=x_rows[t])
-            x_sb.append(x_t)
-
-        def load_chunk(w, first_col, label):
-            by_pass = w.rearrange("(g p j) n -> g p j n", p=P, j=PACK)
-            tiles = []
-            for g in range(PASSES):
-                raw = raw_pool.tile([P, PACK, CHUNK], BF16, name="%s_pass%d" % (label, g))
-                nc.sync.dma_start(out=raw[:], in_=by_pass[g, :, :, first_col : first_col + CHUNK])
-                tiles.append(raw)
-            return tiles
+        ctx.enter_context(tc.manual_schedule())
 
         q_out = out_0.rearrange("b h (p t) d -> p (b h) (t d)", t=S_TILES)
         k_out = out_1.rearrange("b h (p t) d -> p (b h) (t d)", t=S_TILES)
         v_out = out_2.rearrange("b h (p t) d -> p (b h) (t d)", t=S_TILES)
 
-        chunks = []
-        chunks.append((load_chunk(Wk, 0, "wk"), k_out, True))
+        chunks = [
+            (Wk, 0, k_out, True),
+            (Wq, 0 * CHUNK, q_out[:, 0 * HEADS : 1 * HEADS, :], True),
+            (Wq, 1 * CHUNK, q_out[:, 1 * HEADS : 2 * HEADS, :], True),
+            (Wq, 2 * CHUNK, q_out[:, 2 * HEADS : 3 * HEADS, :], True),
+            (Wv, 0, v_out, False),
+            (Wq, 3 * CHUNK, q_out[:, 3 * HEADS : 4 * HEADS, :], True),
+        ]
+        n_chunks = len(chunks)
+
+        w_raw = {}
+        w_grouped = {}
+        w_codes = {}
+        w_scales = {}
+
+        def load(c):
+            w, first_col = chunks[c][0], chunks[c][1]
+            by_pass = w.rearrange("(g p j) n -> g p j n", p=P, j=PACK)
+            for g in range(PASSES):
+                raw = raw_pool.tile([P, PACK, CHUNK], BF16, tag="w_raw")
+                nc.sync.dma_start(out=raw[:], in_=by_pass[g, :, :, first_col : first_col + CHUNK])
+                w_raw[(c, g)] = raw
+
+        def regroup(c):
+            split = CHUNK - VECTOR_COLS
+            for g in range(PASSES):
+                raw = w_raw[(c, g)]
+                grouped = w_group_pool.tile([P, CHUNK, PACK], BF16, tag="w_grouped", align_bytes=64)
+                nc.scalar.copy(
+                    out=grouped[:, 0:split, :].rearrange("p (c i) j -> p c j i", i=4),
+                    in_=raw[:, :, 0:split].rearrange("p j (c i) -> p c j i", i=4),
+                )
+                nc.vector.tensor_copy(
+                    out=grouped[:, split:CHUNK, :].rearrange("p (c i) j -> p c j i", i=4),
+                    in_=raw[:, :, split:CHUNK].rearrange("p j (c i) -> p c j i", i=4),
+                )
+                w_grouped[(c, g)] = grouped
+
+        def quantise(c):
+            codes = w_code_pool.tile([P, PASSES, CHUNK], U32, tag="w_codes", align_bytes=64)
+            scales = w_code_pool.tile([P, PASSES, CHUNK], U8, tag="w_scales", align_bytes=64)
+            for g in range(PASSES):
+                nc.vector.quantize_mx(
+                    out=codes[:, g, :].bitcast(FP8X4),
+                    scales=scales[:, g, :],
+                    in_=w_grouped[(c, g)][:].rearrange("p w j -> p (w j)"),
+                )
+            w_codes[c] = codes
+            w_scales[c] = scales
+
+        def multiply(c):
+            banks = []
+            for t in range(S_TILES):
+                acc = psum.tile([P, CHUNK], F32, tag="bank")
+                for g in range(PASSES):
+                    nc.tensor.matmul_mx(
+                        out=acc[:],
+                        lhsT=x_codes[t][:, g * P : (g + 1) * P].bitcast(FP8X4),
+                        lhsT_scale=x_scales[t][:, g * P : (g + 1) * P],
+                        rhs=w_codes[c][:, g, :].bitcast(FP8X4),
+                        rhs_scale=w_scales[c][:, g, :],
+                        start=(g == 0),
+                        stop=(g == PASSES - 1),
+                    )
+                banks.append(acc)
+            return banks
+
+        def products(acc, t, result):
+            nc.vector.tensor_tensor(
+                out=result[:, :, t, :],
+                in0=acc[:].rearrange("p (h d) -> p h d", h=HEADS),
+                in1=cos_sb[:, t, :].unsqueeze(1).to_broadcast([P, HEADS, DH]),
+                op=MULT,
+            )
+            pairs = acc[:].rearrange("p (h i e) -> p h i e", h=HEADS, e=2)
+            cross = cross_pool.tile([P, 2, HEADS, PAIRS], F32, tag="cross")
+            nc.vector.tensor_tensor(
+                out=cross[:, 0, :, :],
+                in0=pairs[:, :, :, 1],
+                in1=neg_sin_even[:, t, :].unsqueeze(1).to_broadcast([P, HEADS, PAIRS]),
+                op=MULT,
+            )
+            nc.vector.tensor_tensor(
+                out=cross[:, 1, :, :],
+                in0=pairs[:, :, :, 0],
+                in1=sin_odd[:, t, :].unsqueeze(1).to_broadcast([P, HEADS, PAIRS]),
+                op=MULT,
+            )
+            return cross
+
+        def add_cross(engine, cross, t, result):
+            straight = result[:, :, t, :].rearrange("p h (i e) -> p h i e", e=2)
+            engine.tensor_tensor(out=straight, in0=straight, in1=cross[:].rearrange("p e h i -> p h i e"), op=ADD)
+
+        load(0)
+        x_rows = x.rearrange("b (p t) k -> t p (b k)", t=S_TILES)
+        x_sb = []
+        for t in range(S_TILES):
+            x_t = x_pool.tile([P, D], BF16, tag="x_rows")
+            nc.sync.dma_start(out=x_t[:], in_=x_rows[t])
+            x_sb.append(x_t)
         cos_sb = consts.tile([P, S_TILES, DH], BF16)
         sin_sb = consts.tile([P, S_TILES, DH], BF16)
         nc.sync.dma_start(out=cos_sb[:].rearrange("p t d -> p (t d)"), in_=cos.rearrange("(p t) d -> p (t d)", t=S_TILES))
         nc.sync.dma_start(out=sin_sb[:].rearrange("p t d -> p (t d)"), in_=sin.rearrange("(p t) d -> p (t d)", t=S_TILES))
-        for n in range(2048 // CHUNK):
-            chunks.append((load_chunk(Wq, n * CHUNK, "wq%d" % n), q_out[:, n * HEADS : (n + 1) * HEADS, :], True))
-        chunks.append((load_chunk(Wv, 0, "wv"), v_out, False))
-
-        sin_pairs = sin_sb[:].rearrange("p t (i e) -> p t i e", e=2)
-        neg_sin_even = consts.tile([P, S_TILES, PAIRS], F32)
-        sin_odd = consts.tile([P, S_TILES, PAIRS], F32)
-        nc.vector.tensor_scalar_mul(out=neg_sin_even[:], in0=sin_pairs[:, :, :, 0], scalar1=-1.0)
-        nc.vector.tensor_copy(out=sin_odd[:], in_=sin_pairs[:, :, :, 1])
+        for c in range(1, RAW_CHUNKS):
+            load(c)
 
         ident = consts.tile([P, P], F32)
         make_identity(nc, ident[:])
+        sin_pairs = sin_sb[:].rearrange("p t (i e) -> p t i e", e=2)
+        neg_sin_even = consts.tile([P, S_TILES, PAIRS], F32)
+        sin_odd = consts.tile([P, S_TILES, PAIRS], F32)
+        nc.gpsimd.tensor_scalar(out=neg_sin_even[:], in0=sin_pairs[:, :, :, 0], scalar1=-1.0, scalar2=0.0, op0=MULT, op1=ADD)
+        nc.gpsimd.tensor_scalar(out=sin_odd[:], in0=sin_pairs[:, :, :, 1], scalar1=1.0, scalar2=0.0, op0=MULT, op1=ADD)
+
+        regroup(0)
+        quantise(0)
+
         x_codes = []
         x_scales = []
         for t in range(S_TILES):
             words = x_sb[t][:].bitcast(F32).rearrange("s (g w u) -> s g u w", g=PASSES, u=2)
-            grouped_x = x_group_pool.tile([P, PASSES, P, PACK], BF16, align_bytes=64)
+            grouped_x = x_group_pool.tile([P, PASSES, P, PACK], BF16, tag="x_grouped", align_bytes=64)
             grouped_words = grouped_x[:].bitcast(F32)
             for half in range(2):
                 turned = psum.tile([P, 2, 2, P], F32, tag="bank")
@@ -103,95 +190,29 @@ def tile_attention_pa_kernel(tc, x, cos, sin, Wq, Wk, Wv, out_0, out_1, out_2):
             x_codes.append(codes_t)
             x_scales.append(scales_t)
 
-        w_codes = {}
-        w_scales = {}
-        w_grouped = {}
-
-        def regroup(c, g):
-            if g == 0:
-                w_codes[c] = w_code_pool.tile([P, PASSES, CHUNK], U32, name="w_codes", align_bytes=64)
-                w_scales[c] = w_code_pool.tile([P, PASSES, CHUNK], U8, name="w_scales", align_bytes=64)
-            raw = chunks[c][0][g]
-            grouped = w_group_pool.tile([P, CHUNK, PACK], BF16, name="w_grouped", align_bytes=64)
-            split = CHUNK - VECTOR_COLS
-            nc.scalar.copy(
-                out=grouped[:, 0:split, :].rearrange("p (c i) j -> p c j i", i=4),
-                in_=raw[:, :, 0:split].rearrange("p j (c i) -> p c j i", i=4),
-            )
-            nc.vector.tensor_copy(
-                out=grouped[:, split:CHUNK, :].rearrange("p (c i) j -> p c j i", i=4),
-                in_=raw[:, :, split:CHUNK].rearrange("p j (c i) -> p c j i", i=4),
-            )
-            w_grouped[(c, g)] = grouped
-
-        def quantise(c, g):
-            nc.vector.quantize_mx(
-                out=w_codes[c][:, g, :].bitcast(FP8X4),
-                scales=w_scales[c][:, g, :],
-                in_=w_grouped[(c, g)][:].rearrange("p w j -> p (w j)"),
-            )
-
-        def multiply(c):
-            banks = []
-            for t in range(S_TILES):
-                acc = psum.tile([P, CHUNK], F32, tag="bank")
-                for g in range(PASSES):
-                    nc.tensor.matmul_mx(
-                        out=acc[:],
-                        lhsT=x_codes[t][:, g * P : (g + 1) * P].bitcast(FP8X4),
-                        lhsT_scale=x_scales[t][:, g * P : (g + 1) * P],
-                        rhs=w_codes[c][:, g, :].bitcast(FP8X4),
-                        rhs_scale=w_scales[c][:, g, :],
-                        start=(g == 0),
-                        stop=(g == PASSES - 1),
-                    )
-                banks.append(acc)
-            return banks
-
-        def rotate(acc, t, result):
-            straight = result[:, :, t, :]
-            nc.vector.tensor_tensor(
-                out=straight,
-                in0=acc[:].rearrange("p (h d) -> p h d", h=HEADS),
-                in1=cos_sb[:, t, :].unsqueeze(1).to_broadcast([P, HEADS, DH]),
-                op=MULT,
-            )
-            pairs = acc[:].rearrange("p (h i e) -> p h i e", h=HEADS, e=2)
-            cross = cross_pool.tile([P, 2, HEADS, PAIRS], F32)
-            nc.vector.tensor_tensor(
-                out=cross[:, 0, :, :],
-                in0=pairs[:, :, :, 1],
-                in1=neg_sin_even[:, t, :].unsqueeze(1).to_broadcast([P, HEADS, PAIRS]),
-                op=MULT,
-            )
-            nc.vector.tensor_tensor(
-                out=cross[:, 1, :, :],
-                in0=pairs[:, :, :, 0],
-                in1=sin_odd[:, t, :].unsqueeze(1).to_broadcast([P, HEADS, PAIRS]),
-                op=MULT,
-            )
-            nc.gpsimd.tensor_tensor(
-                out=straight.rearrange("p h (i e) -> p h i e", e=2),
-                in0=straight.rearrange("p h (i e) -> p h i e", e=2),
-                in1=cross[:].rearrange("p e h i -> p h i e"),
-                op=ADD,
-            )
-
-        for c in range(AHEAD):
-            for g in range(PASSES):
-                regroup(c, g)
-                quantise(c, g)
-
-        for c in range(len(chunks)):
-            banks = multiply(c)
-            result = result_pool.tile([P, HEADS, S_TILES, DH], F32)
-            for t in range(S_TILES):
-                if c + AHEAD < len(chunks):
-                    regroup(c + AHEAD, t)
-                if chunks[c][2]:
-                    rotate(banks[t], t, result)
-                else:
+        banks = multiply(0)
+        for c in range(n_chunks):
+            rotated = chunks[c][3]
+            result = result_pool.tile([P, HEADS, S_TILES, DH], F32, tag="result")
+            last_cross = None
+            if rotated:
+                for t in range(S_TILES):
+                    cross = products(banks[t], t, result)
+                    if t < S_TILES - 1:
+                        add_cross(nc.gpsimd, cross, t, result)
+                    else:
+                        last_cross = cross
+            next_banks = None
+            if c + 1 < n_chunks:
+                regroup(c + 1)
+                quantise(c + 1)
+                next_banks = multiply(c + 1)
+            if rotated:
+                add_cross(nc.vector, last_cross, S_TILES - 1, result)
+            else:
+                for t in range(S_TILES):
                     nc.scalar.copy(out=result[:, :, t, :], in_=banks[t][:].rearrange("p (h d) -> p h d", h=HEADS))
-                if c + AHEAD < len(chunks):
-                    quantise(c + AHEAD, t)
-            nc.gpsimd.dma_start(out=chunks[c][1], in_=result[:].rearrange("p h t d -> p h (t d)"))
+            if c + RAW_CHUNKS < n_chunks:
+                load(c + RAW_CHUNKS)
+            nc.sync.dma_start(out=chunks[c][2], in_=result[:].rearrange("p h t d -> p h (t d)"))
+            banks = next_banks

@@ -24,6 +24,8 @@ CHUNK = 512
 HEADS = CHUNK // DH
 RAW_CHUNKS = 4
 VECTOR_COLS = 96
+FIRST_VECTOR_COLS = 320
+GPSIMD_TILES = 2
 
 FLOPS = 2 * S * D * (2048 + 512 + 512)
 
@@ -69,8 +71,8 @@ def tile_attention_pa_kernel(tc, x, cos, sin, Wq, Wk, Wv, out_0, out_1, out_2):
                 nc.sync.dma_start(out=raw[:], in_=by_pass[g, :, :, first_col : first_col + CHUNK])
                 w_raw[(c, g)] = raw
 
-        def regroup(c):
-            split = CHUNK - VECTOR_COLS
+        def regroup(c, vector_cols):
+            split = CHUNK - vector_cols
             for g in range(PASSES):
                 raw = w_raw[(c, g)]
                 grouped = w_group_pool.tile([P, CHUNK, PACK], BF16, tag="w_grouped", align_bytes=64)
@@ -84,34 +86,27 @@ def tile_attention_pa_kernel(tc, x, cos, sin, Wq, Wk, Wv, out_0, out_1, out_2):
                 )
                 w_grouped[(c, g)] = grouped
 
-        def quantise(c):
-            codes = w_code_pool.tile([P, PASSES, CHUNK], U32, tag="w_codes", align_bytes=64)
-            scales = w_code_pool.tile([P, PASSES, CHUNK], U8, tag="w_scales", align_bytes=64)
-            for g in range(PASSES):
-                nc.vector.quantize_mx(
-                    out=codes[:, g, :].bitcast(FP8X4),
-                    scales=scales[:, g, :],
-                    in_=w_grouped[(c, g)][:].rearrange("p w j -> p (w j)"),
-                )
-            w_codes[c] = codes
-            w_scales[c] = scales
+        def new_codes(c):
+            w_codes[c] = w_code_pool.tile([P, PASSES, CHUNK], U32, tag="w_codes", name="w_codes", align_bytes=64)
+            w_scales[c] = w_code_pool.tile([P, PASSES, CHUNK], U8, tag="w_scales", name="w_scales", align_bytes=64)
 
-        def multiply(c):
-            banks = []
-            for t in range(S_TILES):
-                acc = psum.tile([P, CHUNK], F32, tag="bank")
-                for g in range(PASSES):
-                    nc.tensor.matmul_mx(
-                        out=acc[:],
-                        lhsT=x_codes[t][:, g * P : (g + 1) * P].bitcast(FP8X4),
-                        lhsT_scale=x_scales[t][:, g * P : (g + 1) * P],
-                        rhs=w_codes[c][:, g, :].bitcast(FP8X4),
-                        rhs_scale=w_scales[c][:, g, :],
-                        start=(g == 0),
-                        stop=(g == PASSES - 1),
-                    )
-                banks.append(acc)
-            return banks
+        def quantise(c, g):
+            nc.vector.quantize_mx(
+                out=w_codes[c][:, g, :].bitcast(FP8X4),
+                scales=w_scales[c][:, g, :],
+                in_=w_grouped[(c, g)][:].rearrange("p w j -> p (w j)"),
+            )
+
+        def multiply(acc, c, t, g):
+            nc.tensor.matmul_mx(
+                out=acc[:],
+                lhsT=x_codes[t][:, g * P : (g + 1) * P].bitcast(FP8X4),
+                lhsT_scale=x_scales[t][:, g * P : (g + 1) * P],
+                rhs=w_codes[c][:, g, :].bitcast(FP8X4),
+                rhs_scale=w_scales[c][:, g, :],
+                start=(g == 0),
+                stop=(g == PASSES - 1),
+            )
 
         def products(acc, t, result):
             nc.vector.tensor_tensor(
@@ -162,24 +157,29 @@ def tile_attention_pa_kernel(tc, x, cos, sin, Wq, Wk, Wv, out_0, out_1, out_2):
         nc.gpsimd.tensor_scalar(out=neg_sin_even[:], in0=sin_pairs[:, :, :, 0], scalar1=-1.0, scalar2=0.0, op0=MULT, op1=ADD)
         nc.gpsimd.tensor_scalar(out=sin_odd[:], in0=sin_pairs[:, :, :, 1], scalar1=1.0, scalar2=0.0, op0=MULT, op1=ADD)
 
-        regroup(0)
-        quantise(0)
+        regroup(0, FIRST_VECTOR_COLS)
+        new_codes(0)
+        for g in range(PASSES):
+            quantise(0, g)
 
         x_codes = []
         x_scales = []
-        for t in range(S_TILES):
+        x_turned = {}
+
+        def transpose_tile(t):
             words = x_sb[t][:].bitcast(F32).rearrange("s (g w u) -> s g u w", g=PASSES, u=2)
-            grouped_x = x_group_pool.tile([P, PASSES, P, PACK], BF16, tag="x_grouped", align_bytes=64)
-            grouped_words = grouped_x[:].bitcast(F32)
             for half in range(2):
                 turned = psum.tile([P, 2, 2, P], F32, tag="bank")
                 for g2 in range(2):
                     for u in range(2):
                         nc.tensor.transpose(turned[:, g2, u, :], words[:, 2 * half + g2, u, :], ident[:])
-                if half == 0:
-                    nc.vector.tensor_copy(out=grouped_words[:, 0:2, :, :], in_=turned[:].rearrange("p g u s -> p g s u"))
-                else:
-                    nc.scalar.copy(out=grouped_words[:, 2:4, :, :], in_=turned[:].rearrange("p g u s -> p g s u"))
+                x_turned[(t, half)] = turned
+
+        def quantise_tile(t):
+            grouped_x = x_group_pool.tile([P, PASSES, P, PACK], BF16, tag="x_grouped", align_bytes=64)
+            grouped_words = grouped_x[:].bitcast(F32)
+            nc.vector.tensor_copy(out=grouped_words[:, 0:2, :, :], in_=x_turned[(t, 0)][:].rearrange("p g u s -> p g s u"))
+            nc.scalar.copy(out=grouped_words[:, 2:4, :, :], in_=x_turned[(t, 1)][:].rearrange("p g u s -> p g s u"))
             codes_t = consts.tile([P, PASSES * P], U32, name="x_codes_%d" % t, align_bytes=64)
             scales_t = consts.tile([P, PASSES * P], U8, name="x_scales_%d" % t, align_bytes=64)
             nc.vector.quantize_mx(
@@ -190,26 +190,42 @@ def tile_attention_pa_kernel(tc, x, cos, sin, Wq, Wk, Wv, out_0, out_1, out_2):
             x_codes.append(codes_t)
             x_scales.append(scales_t)
 
-        banks = multiply(0)
+        banks = []
+        transpose_tile(0)
+        for t in range(S_TILES):
+            if t + 1 < S_TILES:
+                transpose_tile(t + 1)
+            quantise_tile(t)
+            acc = psum.tile([P, CHUNK], F32, tag="bank")
+            for g in range(PASSES):
+                multiply(acc, 0, t, g)
+            banks.append(acc)
+
         for c in range(n_chunks):
             rotated = chunks[c][3]
             result = result_pool.tile([P, HEADS, S_TILES, DH], F32, tag="result")
-            last_cross = None
+            late = []
             if rotated:
                 for t in range(S_TILES):
                     cross = products(banks[t], t, result)
-                    if t < S_TILES - 1:
+                    if t < GPSIMD_TILES:
                         add_cross(nc.gpsimd, cross, t, result)
                     else:
-                        last_cross = cross
-            next_banks = None
+                        late.append((cross, t))
+            next_banks = []
             if c + 1 < n_chunks:
-                regroup(c + 1)
-                quantise(c + 1)
-                next_banks = multiply(c + 1)
-            if rotated:
-                add_cross(nc.vector, last_cross, S_TILES - 1, result)
-            else:
+                regroup(c + 1, VECTOR_COLS)
+                new_codes(c + 1)
+                for t in range(S_TILES):
+                    acc = psum.tile([P, CHUNK], F32, tag="bank")
+                    next_banks.append(acc)
+                for g in range(PASSES):
+                    quantise(c + 1, g)
+                    for t in range(S_TILES):
+                        multiply(next_banks[t], c + 1, t, g)
+            for cross, t in late:
+                add_cross(nc.vector, cross, t, result)
+            if not rotated:
                 for t in range(S_TILES):
                     nc.scalar.copy(out=result[:, :, t, :], in_=banks[t][:].rearrange("p (h d) -> p h d", h=HEADS))
             if c + RAW_CHUNKS < n_chunks:

@@ -22,10 +22,8 @@ S_TILES = S // P
 PASSES = D // K_PASS
 CHUNK = 512
 HEADS = CHUNK // DH
-RAW_CHUNKS = 4
-VECTOR_COLS = 96
-FIRST_VECTOR_COLS = 320
-GPSIMD_TILES = 2
+AHEAD = 2
+VECTOR_COLS = 64
 
 FLOPS = 2 * S * D * (2048 + 512 + 512)
 
@@ -34,61 +32,96 @@ def tile_attention_pa_kernel(tc, x, cos, sin, Wq, Wk, Wv, out_0, out_1, out_2):
     nc = tc.nc
     with ExitStack() as ctx:
         consts = ctx.enter_context(tc.tile_pool(name="consts", bufs=1))
-        x_pool = ctx.enter_context(tc.tile_pool(name="x_rows", bufs=S_TILES))
-        raw_pool = ctx.enter_context(tc.tile_pool(name="raw", bufs=RAW_CHUNKS * PASSES))
+        raw_pool = ctx.enter_context(tc.tile_pool(name="raw", bufs=1))
         x_group_pool = ctx.enter_context(tc.tile_pool(name="x_group", bufs=2))
-        w_group_pool = ctx.enter_context(tc.tile_pool(name="w_group", bufs=2 * PASSES))
-        w_code_pool = ctx.enter_context(tc.tile_pool(name="w_code", bufs=2))
+        w_group_pool = ctx.enter_context(tc.tile_pool(name="w_group", bufs=4))
+        w_code_pool = ctx.enter_context(tc.tile_pool(name="w_code", bufs=AHEAD + 1))
         cross_pool = ctx.enter_context(tc.tile_pool(name="cross", bufs=4))
-        result_pool = ctx.enter_context(tc.tile_pool(name="result", bufs=4))
+        result_pool = ctx.enter_context(tc.tile_pool(name="result", bufs=3))
         psum = ctx.enter_context(tc.psum_pool(name="psum", bufs=8))
-        ctx.enter_context(tc.manual_schedule())
+
+        def load_chunk(w, first_col, label):
+            by_pass = w.rearrange("(g p j) n -> g p j n", p=P, j=PACK)
+            tiles = []
+            for g in range(PASSES):
+                raw = raw_pool.tile([P, PACK, CHUNK], BF16, name="%s_pass%d" % (label, g))
+                nc.sync.dma_start(out=raw[:], in_=by_pass[g, :, :, first_col : first_col + CHUNK])
+                tiles.append(raw)
+            return tiles
 
         q_out = out_0.rearrange("b h (p t) d -> p (b h) (t d)", t=S_TILES)
         k_out = out_1.rearrange("b h (p t) d -> p (b h) (t d)", t=S_TILES)
         v_out = out_2.rearrange("b h (p t) d -> p (b h) (t d)", t=S_TILES)
 
-        chunks = [
-            (Wk, 0, k_out, True),
-            (Wq, 0 * CHUNK, q_out[:, 0 * HEADS : 1 * HEADS, :], True),
-            (Wq, 1 * CHUNK, q_out[:, 1 * HEADS : 2 * HEADS, :], True),
-            (Wq, 2 * CHUNK, q_out[:, 2 * HEADS : 3 * HEADS, :], True),
-            (Wv, 0, v_out, False),
-            (Wq, 3 * CHUNK, q_out[:, 3 * HEADS : 4 * HEADS, :], True),
-        ]
-        n_chunks = len(chunks)
+        chunks = []
+        chunks.append((load_chunk(Wk, 0, "wk"), k_out, True))
+        x_rows = x.rearrange("b (p t) k -> t p (b k)", t=S_TILES)
+        x_sb = []
+        for t in range(S_TILES):
+            x_t = raw_pool.tile([P, D], BF16, name="x_rows_%d" % t)
+            nc.sync.dma_start(out=x_t[:], in_=x_rows[t])
+            x_sb.append(x_t)
+        cos_sb = consts.tile([P, S_TILES, DH], BF16)
+        sin_sb = consts.tile([P, S_TILES, DH], BF16)
+        nc.sync.dma_start(out=cos_sb[:].rearrange("p t d -> p (t d)"), in_=cos.rearrange("(p t) d -> p (t d)", t=S_TILES))
+        nc.sync.dma_start(out=sin_sb[:].rearrange("p t d -> p (t d)"), in_=sin.rearrange("(p t) d -> p (t d)", t=S_TILES))
+        for n in range(2048 // CHUNK):
+            chunks.append((load_chunk(Wq, n * CHUNK, "wq%d" % n), q_out[:, n * HEADS : (n + 1) * HEADS, :], True))
+        chunks.append((load_chunk(Wv, 0, "wv"), v_out, False))
 
-        w_raw = {}
-        w_grouped = {}
+        sin_pairs = sin_sb[:].rearrange("p t (i e) -> p t i e", e=2)
+        neg_sin_even = consts.tile([P, S_TILES, PAIRS], F32)
+        sin_odd = consts.tile([P, S_TILES, PAIRS], F32)
+        nc.gpsimd.tensor_scalar(out=neg_sin_even[:], in0=sin_pairs[:, :, :, 0], scalar1=-1.0, scalar2=0.0, op0=MULT, op1=ADD)
+        nc.gpsimd.tensor_scalar(out=sin_odd[:], in0=sin_pairs[:, :, :, 1], scalar1=1.0, scalar2=0.0, op0=MULT, op1=ADD)
+
+        ident = consts.tile([P, P], F32)
+        make_identity(nc, ident[:])
+        x_codes = []
+        x_scales = []
+        for t in range(S_TILES):
+            words = x_sb[t][:].bitcast(F32).rearrange("s (g w u) -> s g u w", g=PASSES, u=2)
+            grouped_x = x_group_pool.tile([P, PASSES, P, PACK], BF16, align_bytes=64)
+            grouped_words = grouped_x[:].bitcast(F32)
+            for half in range(2):
+                turned = psum.tile([P, 2, 2, P], F32, tag="bank")
+                for g2 in range(2):
+                    for u in range(2):
+                        nc.tensor.transpose(turned[:, g2, u, :], words[:, 2 * half + g2, u, :], ident[:])
+                if half == 0:
+                    nc.vector.tensor_copy(out=grouped_words[:, 0:2, :, :], in_=turned[:].rearrange("p g u s -> p g s u"))
+                else:
+                    nc.scalar.copy(out=grouped_words[:, 2:4, :, :], in_=turned[:].rearrange("p g u s -> p g s u"))
+            codes_t = consts.tile([P, PASSES * P], U32, name="x_codes_%d" % t, align_bytes=64)
+            scales_t = consts.tile([P, PASSES * P], U8, name="x_scales_%d" % t, align_bytes=64)
+            nc.vector.quantize_mx(
+                out=codes_t[:].bitcast(FP8X4),
+                scales=scales_t[:],
+                in_=grouped_x[:].rearrange("p g s j -> p (g s j)"),
+            )
+            x_codes.append(codes_t)
+            x_scales.append(scales_t)
+
         w_codes = {}
         w_scales = {}
+        w_grouped = {}
 
-        def load(c):
-            w, first_col = chunks[c][0], chunks[c][1]
-            by_pass = w.rearrange("(g p j) n -> g p j n", p=P, j=PACK)
-            for g in range(PASSES):
-                raw = raw_pool.tile([P, PACK, CHUNK], BF16, tag="w_raw")
-                nc.sync.dma_start(out=raw[:], in_=by_pass[g, :, :, first_col : first_col + CHUNK])
-                w_raw[(c, g)] = raw
-
-        def regroup(c, vector_cols):
-            split = CHUNK - vector_cols
-            for g in range(PASSES):
-                raw = w_raw[(c, g)]
-                grouped = w_group_pool.tile([P, CHUNK, PACK], BF16, tag="w_grouped", align_bytes=64)
-                nc.scalar.copy(
-                    out=grouped[:, 0:split, :].rearrange("p (c i) j -> p c j i", i=4),
-                    in_=raw[:, :, 0:split].rearrange("p j (c i) -> p c j i", i=4),
-                )
-                nc.vector.tensor_copy(
-                    out=grouped[:, split:CHUNK, :].rearrange("p (c i) j -> p c j i", i=4),
-                    in_=raw[:, :, split:CHUNK].rearrange("p j (c i) -> p c j i", i=4),
-                )
-                w_grouped[(c, g)] = grouped
-
-        def new_codes(c):
-            w_codes[c] = w_code_pool.tile([P, PASSES, CHUNK], U32, tag="w_codes", name="w_codes", align_bytes=64)
-            w_scales[c] = w_code_pool.tile([P, PASSES, CHUNK], U8, tag="w_scales", name="w_scales", align_bytes=64)
+        def regroup(c, g):
+            if g == 0:
+                w_codes[c] = w_code_pool.tile([P, PASSES, CHUNK], U32, name="w_codes", align_bytes=64)
+                w_scales[c] = w_code_pool.tile([P, PASSES, CHUNK], U8, name="w_scales", align_bytes=64)
+            raw = chunks[c][0][g]
+            grouped = w_group_pool.tile([P, CHUNK, PACK], BF16, name="w_grouped", align_bytes=64)
+            split = CHUNK - VECTOR_COLS
+            nc.scalar.copy(
+                out=grouped[:, 0:split, :].rearrange("p (c i) j -> p c j i", i=4),
+                in_=raw[:, :, 0:split].rearrange("p j (c i) -> p c j i", i=4),
+            )
+            nc.vector.tensor_copy(
+                out=grouped[:, split:CHUNK, :].rearrange("p (c i) j -> p c j i", i=4),
+                in_=raw[:, :, split:CHUNK].rearrange("p j (c i) -> p c j i", i=4),
+            )
+            w_grouped[(c, g)] = grouped
 
         def quantise(c, g):
             nc.vector.quantize_mx(
@@ -97,26 +130,33 @@ def tile_attention_pa_kernel(tc, x, cos, sin, Wq, Wk, Wv, out_0, out_1, out_2):
                 in_=w_grouped[(c, g)][:].rearrange("p w j -> p (w j)"),
             )
 
-        def multiply(acc, c, t, g):
-            nc.tensor.matmul_mx(
-                out=acc[:],
-                lhsT=x_codes[t][:, g * P : (g + 1) * P].bitcast(FP8X4),
-                lhsT_scale=x_scales[t][:, g * P : (g + 1) * P],
-                rhs=w_codes[c][:, g, :].bitcast(FP8X4),
-                rhs_scale=w_scales[c][:, g, :],
-                start=(g == 0),
-                stop=(g == PASSES - 1),
-            )
+        def multiply(c):
+            banks = []
+            for t in range(S_TILES):
+                acc = psum.tile([P, CHUNK], F32, tag="bank")
+                for g in range(PASSES):
+                    nc.tensor.matmul_mx(
+                        out=acc[:],
+                        lhsT=x_codes[t][:, g * P : (g + 1) * P].bitcast(FP8X4),
+                        lhsT_scale=x_scales[t][:, g * P : (g + 1) * P],
+                        rhs=w_codes[c][:, g, :].bitcast(FP8X4),
+                        rhs_scale=w_scales[c][:, g, :],
+                        start=(g == 0),
+                        stop=(g == PASSES - 1),
+                    )
+                banks.append(acc)
+            return banks
 
-        def products(acc, t, result):
+        def rotate(acc, t, result):
+            straight = result[:, :, t, :]
             nc.vector.tensor_tensor(
-                out=result[:, :, t, :],
+                out=straight,
                 in0=acc[:].rearrange("p (h d) -> p h d", h=HEADS),
                 in1=cos_sb[:, t, :].unsqueeze(1).to_broadcast([P, HEADS, DH]),
                 op=MULT,
             )
             pairs = acc[:].rearrange("p (h i e) -> p h i e", h=HEADS, e=2)
-            cross = cross_pool.tile([P, 2, HEADS, PAIRS], F32, tag="cross")
+            cross = cross_pool.tile([P, 2, HEADS, PAIRS], F32)
             nc.vector.tensor_tensor(
                 out=cross[:, 0, :, :],
                 in0=pairs[:, :, :, 1],
@@ -129,106 +169,28 @@ def tile_attention_pa_kernel(tc, x, cos, sin, Wq, Wk, Wv, out_0, out_1, out_2):
                 in1=sin_odd[:, t, :].unsqueeze(1).to_broadcast([P, HEADS, PAIRS]),
                 op=MULT,
             )
-            return cross
-
-        def add_cross(engine, cross, t, result):
-            straight = result[:, :, t, :].rearrange("p h (i e) -> p h i e", e=2)
-            engine.tensor_tensor(out=straight, in0=straight, in1=cross[:].rearrange("p e h i -> p h i e"), op=ADD)
-
-        load(0)
-        x_rows = x.rearrange("b (p t) k -> t p (b k)", t=S_TILES)
-        x_sb = []
-        for t in range(S_TILES):
-            x_t = x_pool.tile([P, D], BF16, tag="x_rows")
-            nc.sync.dma_start(out=x_t[:], in_=x_rows[t])
-            x_sb.append(x_t)
-        cos_sb = consts.tile([P, S_TILES, DH], BF16)
-        sin_sb = consts.tile([P, S_TILES, DH], BF16)
-        nc.sync.dma_start(out=cos_sb[:].rearrange("p t d -> p (t d)"), in_=cos.rearrange("(p t) d -> p (t d)", t=S_TILES))
-        nc.sync.dma_start(out=sin_sb[:].rearrange("p t d -> p (t d)"), in_=sin.rearrange("(p t) d -> p (t d)", t=S_TILES))
-        for c in range(1, RAW_CHUNKS):
-            load(c)
-
-        ident = consts.tile([P, P], F32)
-        make_identity(nc, ident[:])
-        sin_pairs = sin_sb[:].rearrange("p t (i e) -> p t i e", e=2)
-        neg_sin_even = consts.tile([P, S_TILES, PAIRS], F32)
-        sin_odd = consts.tile([P, S_TILES, PAIRS], F32)
-        nc.gpsimd.tensor_scalar(out=neg_sin_even[:], in0=sin_pairs[:, :, :, 0], scalar1=-1.0, scalar2=0.0, op0=MULT, op1=ADD)
-        nc.gpsimd.tensor_scalar(out=sin_odd[:], in0=sin_pairs[:, :, :, 1], scalar1=1.0, scalar2=0.0, op0=MULT, op1=ADD)
-
-        regroup(0, FIRST_VECTOR_COLS)
-        new_codes(0)
-        for g in range(PASSES):
-            quantise(0, g)
-
-        x_codes = []
-        x_scales = []
-        x_turned = {}
-
-        def transpose_tile(t):
-            words = x_sb[t][:].bitcast(F32).rearrange("s (g w u) -> s g u w", g=PASSES, u=2)
-            for half in range(2):
-                turned = psum.tile([P, 2, 2, P], F32, tag="bank")
-                for g2 in range(2):
-                    for u in range(2):
-                        nc.tensor.transpose(turned[:, g2, u, :], words[:, 2 * half + g2, u, :], ident[:])
-                x_turned[(t, half)] = turned
-
-        def quantise_tile(t):
-            grouped_x = x_group_pool.tile([P, PASSES, P, PACK], BF16, tag="x_grouped", align_bytes=64)
-            grouped_words = grouped_x[:].bitcast(F32)
-            nc.vector.tensor_copy(out=grouped_words[:, 0:2, :, :], in_=x_turned[(t, 0)][:].rearrange("p g u s -> p g s u"))
-            nc.scalar.copy(out=grouped_words[:, 2:4, :, :], in_=x_turned[(t, 1)][:].rearrange("p g u s -> p g s u"))
-            codes_t = consts.tile([P, PASSES * P], U32, name="x_codes_%d" % t, align_bytes=64)
-            scales_t = consts.tile([P, PASSES * P], U8, name="x_scales_%d" % t, align_bytes=64)
-            nc.vector.quantize_mx(
-                out=codes_t[:].bitcast(FP8X4),
-                scales=scales_t[:],
-                in_=grouped_x[:].rearrange("p g s j -> p (g s j)"),
+            nc.vector.tensor_tensor(
+                out=straight.rearrange("p h (i e) -> p h i e", e=2),
+                in0=straight.rearrange("p h (i e) -> p h i e", e=2),
+                in1=cross[:].rearrange("p e h i -> p h i e"),
+                op=ADD,
             )
-            x_codes.append(codes_t)
-            x_scales.append(scales_t)
 
-        banks = []
-        transpose_tile(0)
-        for t in range(S_TILES):
-            if t + 1 < S_TILES:
-                transpose_tile(t + 1)
-            quantise_tile(t)
-            acc = psum.tile([P, CHUNK], F32, tag="bank")
+        for c in range(AHEAD):
             for g in range(PASSES):
-                multiply(acc, 0, t, g)
-            banks.append(acc)
+                regroup(c, g)
+                quantise(c, g)
 
-        for c in range(n_chunks):
-            rotated = chunks[c][3]
-            result = result_pool.tile([P, HEADS, S_TILES, DH], F32, tag="result")
-            late = []
-            if rotated:
-                for t in range(S_TILES):
-                    cross = products(banks[t], t, result)
-                    if t < GPSIMD_TILES:
-                        add_cross(nc.gpsimd, cross, t, result)
-                    else:
-                        late.append((cross, t))
-            next_banks = []
-            if c + 1 < n_chunks:
-                regroup(c + 1, VECTOR_COLS)
-                new_codes(c + 1)
-                for t in range(S_TILES):
-                    acc = psum.tile([P, CHUNK], F32, tag="bank")
-                    next_banks.append(acc)
-                for g in range(PASSES):
-                    quantise(c + 1, g)
-                    for t in range(S_TILES):
-                        multiply(next_banks[t], c + 1, t, g)
-            for cross, t in late:
-                add_cross(nc.vector, cross, t, result)
-            if not rotated:
-                for t in range(S_TILES):
+        for c in range(len(chunks)):
+            banks = multiply(c)
+            result = result_pool.tile([P, HEADS, S_TILES, DH], F32)
+            for t in range(S_TILES):
+                if c + AHEAD < len(chunks):
+                    regroup(c + AHEAD, t)
+                if chunks[c][2]:
+                    rotate(banks[t], t, result)
+                else:
                     nc.scalar.copy(out=result[:, :, t, :], in_=banks[t][:].rearrange("p (h d) -> p h d", h=HEADS))
-            if c + RAW_CHUNKS < n_chunks:
-                load(c + RAW_CHUNKS)
-            nc.sync.dma_start(out=chunks[c][2], in_=result[:].rearrange("p h t d -> p h (t d)"))
-            banks = next_banks
+                if c + AHEAD < len(chunks):
+                    quantise(c + AHEAD, t)
+            nc.sync.dma_start(out=chunks[c][1], in_=result[:].rearrange("p h t d -> p h (t d)"))

@@ -23,7 +23,7 @@ PASSES = D // K_PASS
 CHUNK = 512
 HEADS = CHUNK // DH
 AHEAD = 2
-VECTOR_COLS = 64
+VECTOR_COLS = (256, 128, 0, 0, 0, 0)
 
 FLOPS = 2 * S * D * (2048 + 512 + 512)
 
@@ -40,46 +40,56 @@ def tile_attention_pa_kernel(tc, x, cos, sin, Wq, Wk, Wv, out_0, out_1, out_2):
         result_pool = ctx.enter_context(tc.tile_pool(name="result", bufs=3))
         psum = ctx.enter_context(tc.psum_pool(name="psum", bufs=8))
 
-        def load_chunk(w, first_col, label):
+        def load_passes(w, first_col, label, passes):
             by_pass = w.rearrange("(g p j) n -> g p j n", p=P, j=PACK)
             tiles = []
-            for g in range(PASSES):
+            for g in passes:
                 raw = raw_pool.tile([P, PACK, CHUNK], BF16, name="%s_pass%d" % (label, g))
                 nc.sync.dma_start(out=raw[:], in_=by_pass[g, :, :, first_col : first_col + CHUNK])
                 tiles.append(raw)
             return tiles
 
-        q_out = out_0.rearrange("b h (p t) d -> p (b h) (t d)", t=S_TILES)
-        k_out = out_1.rearrange("b h (p t) d -> p (b h) (t d)", t=S_TILES)
-        v_out = out_2.rearrange("b h (p t) d -> p (b h) (t d)", t=S_TILES)
+        def load_chunk(w, first_col, label):
+            return load_passes(w, first_col, label, range(PASSES))
+
+        q_out = out_0.rearrange("b h (p t) d -> p (b h) t d", t=S_TILES)
+        k_out = out_1.rearrange("b h (p t) d -> p (b h) t d", t=S_TILES)
+        v_out = out_2.rearrange("b h (p t) d -> p (b h) t d", t=S_TILES)
 
         chunks = []
-        chunks.append((load_chunk(Wk, 0, "wk"), k_out, True))
         x_rows = x.rearrange("b (p t) k -> t p (b k)", t=S_TILES)
         x_sb = []
-        for t in range(S_TILES):
+
+        def load_x(t):
             x_t = raw_pool.tile([P, D], BF16, name="x_rows_%d" % t)
             nc.sync.dma_start(out=x_t[:], in_=x_rows[t])
             x_sb.append(x_t)
+
+        wk_tiles = load_passes(Wk, 0, "wk", range(0, 2))
+        load_x(0)
+        wk_tiles.extend(load_passes(Wk, 0, "wk", range(2, PASSES)))
+        chunks.append((wk_tiles, k_out, True))
         cos_sb = consts.tile([P, S_TILES, DH], BF16)
         sin_sb = consts.tile([P, S_TILES, DH], BF16)
-        nc.sync.dma_start(out=cos_sb[:].rearrange("p t d -> p (t d)"), in_=cos.rearrange("(p t) d -> p (t d)", t=S_TILES))
         nc.sync.dma_start(out=sin_sb[:].rearrange("p t d -> p (t d)"), in_=sin.rearrange("(p t) d -> p (t d)", t=S_TILES))
+        nc.sync.dma_start(out=cos_sb[:].rearrange("p t d -> p (t d)"), in_=cos.rearrange("(p t) d -> p (t d)", t=S_TILES))
+        for t in range(1, S_TILES):
+            load_x(t)
         for n in range(2048 // CHUNK):
-            chunks.append((load_chunk(Wq, n * CHUNK, "wq%d" % n), q_out[:, n * HEADS : (n + 1) * HEADS, :], True))
+            chunks.append((load_chunk(Wq, n * CHUNK, "wq%d" % n), q_out[:, n * HEADS : (n + 1) * HEADS, :, :], True))
         chunks.append((load_chunk(Wv, 0, "wv"), v_out, False))
 
         sin_pairs = sin_sb[:].rearrange("p t (i e) -> p t i e", e=2)
-        neg_sin_even = consts.tile([P, S_TILES, PAIRS], F32)
-        sin_odd = consts.tile([P, S_TILES, PAIRS], F32)
-        nc.gpsimd.tensor_scalar(out=neg_sin_even[:], in0=sin_pairs[:, :, :, 0], scalar1=-1.0, scalar2=0.0, op0=MULT, op1=ADD)
-        nc.gpsimd.tensor_scalar(out=sin_odd[:], in0=sin_pairs[:, :, :, 1], scalar1=1.0, scalar2=0.0, op0=MULT, op1=ADD)
+        signed_sin = consts.tile([P, S_TILES, PAIRS, 2], F32)
+        nc.gpsimd.tensor_scalar(out=signed_sin[:, :, :, 0], in0=sin_pairs[:, :, :, 0], scalar1=-1.0, scalar2=0.0, op0=MULT, op1=ADD)
+        nc.gpsimd.tensor_scalar(out=signed_sin[:, :, :, 1], in0=sin_pairs[:, :, :, 1], scalar1=1.0, scalar2=0.0, op0=MULT, op1=ADD)
 
         ident = consts.tile([P, P], F32)
         make_identity(nc, ident[:])
         x_codes = []
         x_scales = []
-        for t in range(S_TILES):
+
+        def turn_x(t):
             words = x_sb[t][:].bitcast(F32).rearrange("s (g w u) -> s g u w", g=PASSES, u=2)
             grouped_x = x_group_pool.tile([P, PASSES, P, PACK], BF16, align_bytes=64)
             grouped_words = grouped_x[:].bitcast(F32)
@@ -88,10 +98,10 @@ def tile_attention_pa_kernel(tc, x, cos, sin, Wq, Wk, Wv, out_0, out_1, out_2):
                 for g2 in range(2):
                     for u in range(2):
                         nc.tensor.transpose(turned[:, g2, u, :], words[:, 2 * half + g2, u, :], ident[:])
-                if half == 0:
-                    nc.vector.tensor_copy(out=grouped_words[:, 0:2, :, :], in_=turned[:].rearrange("p g u s -> p g s u"))
-                else:
-                    nc.scalar.copy(out=grouped_words[:, 2:4, :, :], in_=turned[:].rearrange("p g u s -> p g s u"))
+                nc.scalar.copy(
+                    out=grouped_words[:, 2 * half : 2 * half + 2, :, :],
+                    in_=turned[:].rearrange("p g u s -> p g s u"),
+                )
             codes_t = consts.tile([P, PASSES * P], U32, name="x_codes_%d" % t, align_bytes=64)
             scales_t = consts.tile([P, PASSES * P], U8, name="x_scales_%d" % t, align_bytes=64)
             nc.vector.quantize_mx(
@@ -112,15 +122,16 @@ def tile_attention_pa_kernel(tc, x, cos, sin, Wq, Wk, Wv, out_0, out_1, out_2):
                 w_scales[c] = w_code_pool.tile([P, PASSES, CHUNK], U8, name="w_scales", align_bytes=64)
             raw = chunks[c][0][g]
             grouped = w_group_pool.tile([P, CHUNK, PACK], BF16, name="w_grouped", align_bytes=64)
-            split = CHUNK - VECTOR_COLS
+            split = CHUNK - VECTOR_COLS[c]
             nc.scalar.copy(
                 out=grouped[:, 0:split, :].rearrange("p (c i) j -> p c j i", i=4),
                 in_=raw[:, :, 0:split].rearrange("p j (c i) -> p c j i", i=4),
             )
-            nc.vector.tensor_copy(
-                out=grouped[:, split:CHUNK, :].rearrange("p (c i) j -> p c j i", i=4),
-                in_=raw[:, :, split:CHUNK].rearrange("p j (c i) -> p c j i", i=4),
-            )
+            if split < CHUNK:
+                nc.vector.tensor_copy(
+                    out=grouped[:, split:CHUNK, :].rearrange("p (c i) j -> p c j i", i=4),
+                    in_=raw[:, :, split:CHUNK].rearrange("p j (c i) -> p c j i", i=4),
+                )
             w_grouped[(c, g)] = grouped
 
         def quantise(c, g):
@@ -155,32 +166,40 @@ def tile_attention_pa_kernel(tc, x, cos, sin, Wq, Wk, Wv, out_0, out_1, out_2):
                 in1=cos_sb[:, t, :].unsqueeze(1).to_broadcast([P, HEADS, DH]),
                 op=MULT,
             )
-            pairs = acc[:].rearrange("p (h i e) -> p h i e", h=HEADS, e=2)
-            cross = cross_pool.tile([P, 2, HEADS, PAIRS], F32)
+            swapped = acc[:].rearrange("p (h i e) -> p h i e", h=HEADS, e=2)[:, :, :, ::-1]
+            cross = cross_pool.tile([P, HEADS, PAIRS, 2], F32)
             nc.vector.tensor_tensor(
-                out=cross[:, 0, :, :],
-                in0=pairs[:, :, :, 1],
-                in1=neg_sin_even[:, t, :].unsqueeze(1).to_broadcast([P, HEADS, PAIRS]),
+                out=cross[:],
+                in0=swapped,
+                in1=signed_sin[:, t, :, :].unsqueeze(1).to_broadcast([P, HEADS, PAIRS, 2]),
                 op=MULT,
             )
             nc.vector.tensor_tensor(
-                out=cross[:, 1, :, :],
-                in0=pairs[:, :, :, 0],
-                in1=sin_odd[:, t, :].unsqueeze(1).to_broadcast([P, HEADS, PAIRS]),
-                op=MULT,
-            )
-            nc.vector.tensor_tensor(
-                out=straight.rearrange("p h (i e) -> p h i e", e=2),
-                in0=straight.rearrange("p h (i e) -> p h i e", e=2),
-                in1=cross[:].rearrange("p e h i -> p h i e"),
+                out=straight,
+                in0=straight,
+                in1=cross[:].rearrange("p h i e -> p h (i e)"),
                 op=ADD,
             )
 
-        for c in range(AHEAD):
+        for g in range(PASSES):
+            if g == 2:
+                turn_x(0)
+            regroup(0, g)
+            quantise(0, g)
+        for t in range(1, S_TILES):
+            turn_x(t)
+        for c in range(1, AHEAD):
             for g in range(PASSES):
                 regroup(c, g)
                 quantise(c, g)
 
+        def store(c, result, first_tile, end_tile):
+            nc.sync.dma_start(
+                out=chunks[c][1][:, :, first_tile:end_tile, :].rearrange("p h t d -> p h (t d)"),
+                in_=result[:, :, first_tile:end_tile, :].rearrange("p h t d -> p h (t d)"),
+            )
+
+        last_rotated = max(c for c in range(len(chunks)) if chunks[c][2])
         for c in range(len(chunks)):
             banks = multiply(c)
             result = result_pool.tile([P, HEADS, S_TILES, DH], F32)
@@ -193,4 +212,7 @@ def tile_attention_pa_kernel(tc, x, cos, sin, Wq, Wk, Wv, out_0, out_1, out_2):
                     nc.scalar.copy(out=result[:, :, t, :], in_=banks[t][:].rearrange("p (h d) -> p h d", h=HEADS))
                 if c + AHEAD < len(chunks):
                     quantise(c + AHEAD, t)
-            nc.sync.dma_start(out=chunks[c][1], in_=result[:].rearrange("p h t d -> p h (t d)"))
+                if c >= last_rotated:
+                    store(c, result, t, t + 1)
+            if c < last_rotated:
+                store(c, result, 0, S_TILES)

@@ -98,10 +98,16 @@ def tile_attention_pa_kernel(tc, x, cos, sin, Wq, Wk, Wv, out_0, out_1, out_2):
                 for g2 in range(2):
                     for u in range(2):
                         nc.tensor.transpose(turned[:, g2, u, :], words[:, 2 * half + g2, u, :], ident[:])
-                nc.scalar.copy(
-                    out=grouped_words[:, 2 * half : 2 * half + 2, :, :],
-                    in_=turned[:].rearrange("p g u s -> p g s u"),
-                )
+                if t >= 2 and half == 0:
+                    nc.vector.tensor_copy(
+                        out=grouped_words[:, 2 * half : 2 * half + 2, :, :],
+                        in_=turned[:].rearrange("p g u s -> p g s u"),
+                    )
+                else:
+                    nc.scalar.copy(
+                        out=grouped_words[:, 2 * half : 2 * half + 2, :, :],
+                        in_=turned[:].rearrange("p g u s -> p g s u"),
+                    )
             codes_t = consts.tile([P, PASSES * P], U32, name="x_codes_%d" % t, align_bytes=64)
             scales_t = consts.tile([P, PASSES * P], U8, name="x_scales_%d" % t, align_bytes=64)
             nc.vector.quantize_mx(
@@ -145,17 +151,21 @@ def tile_attention_pa_kernel(tc, x, cos, sin, Wq, Wk, Wv, out_0, out_1, out_2):
             banks = []
             for t in range(S_TILES):
                 acc = psum.tile([P, CHUNK], F32, tag="bank")
-                for g in range(PASSES):
-                    nc.tensor.matmul_mx(
-                        out=acc[:],
-                        lhsT=x_codes[t][:, g * P : (g + 1) * P].bitcast(FP8X4),
-                        lhsT_scale=x_scales[t][:, g * P : (g + 1) * P],
-                        rhs=w_codes[c][:, g, :].bitcast(FP8X4),
-                        rhs_scale=w_scales[c][:, g, :],
-                        start=(g == 0),
-                        stop=(g == PASSES - 1),
-                    )
                 banks.append(acc)
+            if c == len(chunks) - 1:
+                order = [(t, g) for g in range(PASSES) for t in range(S_TILES)]
+            else:
+                order = [(t, g) for t in range(S_TILES) for g in range(PASSES)]
+            for t, g in order:
+                nc.tensor.matmul_mx(
+                    out=banks[t][:],
+                    lhsT=x_codes[t][:, g * P : (g + 1) * P].bitcast(FP8X4),
+                    lhsT_scale=x_scales[t][:, g * P : (g + 1) * P],
+                    rhs=w_codes[c][:, g, :].bitcast(FP8X4),
+                    rhs_scale=w_scales[c][:, g, :],
+                    start=(g == 0),
+                    stop=(g == PASSES - 1),
+                )
             return banks
 
         def rotate(acc, t, result):

@@ -23,7 +23,8 @@ PASSES = D // K_PASS
 CHUNK = 512
 HEADS = CHUNK // DH
 AHEAD = 2
-VECTOR_COLS = (256, 128, 0, 0, 0, 0)
+VECTOR_COLS = (320, 64, 0, 0, 0, 0)
+GPSIMD_COLS = (0, 96, 96, 96, 96, 96)
 
 FLOPS = 2 * S * D * (2048 + 512 + 512)
 
@@ -89,31 +90,36 @@ def tile_attention_pa_kernel(tc, x, cos, sin, Wq, Wk, Wv, out_0, out_1, out_2):
         x_codes = []
         x_scales = []
 
-        def turn_x(t):
+        x_banks = {}
+        x_grouped = {}
+
+        def transpose_x(t):
             words = x_sb[t][:].bitcast(F32).rearrange("s (g w u) -> s g u w", g=PASSES, u=2)
-            grouped_x = x_group_pool.tile([P, PASSES, P, PACK], BF16, align_bytes=64)
-            grouped_words = grouped_x[:].bitcast(F32)
+            x_banks[t] = []
             for half in range(2):
                 turned = psum.tile([P, 2, 2, P], F32, tag="bank")
+                x_banks[t].append(turned)
                 for g2 in range(2):
                     for u in range(2):
                         nc.tensor.transpose(turned[:, g2, u, :], words[:, 2 * half + g2, u, :], ident[:])
-                if t >= 2 and half == 0:
-                    nc.vector.tensor_copy(
-                        out=grouped_words[:, 2 * half : 2 * half + 2, :, :],
-                        in_=turned[:].rearrange("p g u s -> p g s u"),
-                    )
-                else:
-                    nc.scalar.copy(
-                        out=grouped_words[:, 2 * half : 2 * half + 2, :, :],
-                        in_=turned[:].rearrange("p g u s -> p g s u"),
-                    )
+
+        def copy_x(t):
+            grouped_x = x_group_pool.tile([P, PASSES, P, PACK], BF16, align_bytes=64)
+            x_grouped[t] = grouped_x
+            grouped_words = grouped_x[:].bitcast(F32)
+            for half in range(2):
+                nc.scalar.copy(
+                    out=grouped_words[:, 2 * half : 2 * half + 2, :, :],
+                    in_=x_banks[t][half][:].rearrange("p g u s -> p g s u"),
+                )
+
+        def quantise_x(t):
             codes_t = consts.tile([P, PASSES * P], U32, name="x_codes_%d" % t, align_bytes=64)
             scales_t = consts.tile([P, PASSES * P], U8, name="x_scales_%d" % t, align_bytes=64)
             nc.vector.quantize_mx(
                 out=codes_t[:].bitcast(FP8X4),
                 scales=scales_t[:],
-                in_=grouped_x[:].rearrange("p g s j -> p (g s j)"),
+                in_=x_grouped[t][:].rearrange("p g s j -> p (g s j)"),
             )
             x_codes.append(codes_t)
             x_scales.append(scales_t)
@@ -128,15 +134,25 @@ def tile_attention_pa_kernel(tc, x, cos, sin, Wq, Wk, Wv, out_0, out_1, out_2):
                 w_scales[c] = w_code_pool.tile([P, PASSES, CHUNK], U8, name="w_scales", align_bytes=64)
             raw = chunks[c][0][g]
             grouped = w_group_pool.tile([P, CHUNK, PACK], BF16, name="w_grouped", align_bytes=64)
-            split = CHUNK - VECTOR_COLS[c]
+            gpsimd_from = CHUNK - GPSIMD_COLS[c]
+            split = gpsimd_from - VECTOR_COLS[c]
             nc.scalar.copy(
                 out=grouped[:, 0:split, :].rearrange("p (c i) j -> p c j i", i=4),
                 in_=raw[:, :, 0:split].rearrange("p j (c i) -> p c j i", i=4),
             )
-            if split < CHUNK:
+            if split < gpsimd_from:
                 nc.vector.tensor_copy(
-                    out=grouped[:, split:CHUNK, :].rearrange("p (c i) j -> p c j i", i=4),
-                    in_=raw[:, :, split:CHUNK].rearrange("p j (c i) -> p c j i", i=4),
+                    out=grouped[:, split:gpsimd_from, :].rearrange("p (c i) j -> p c j i", i=4),
+                    in_=raw[:, :, split:gpsimd_from].rearrange("p j (c i) -> p c j i", i=4),
+                )
+            if gpsimd_from < CHUNK:
+                nc.gpsimd.tensor_scalar(
+                    out=grouped[:, gpsimd_from:CHUNK, :],
+                    in0=raw[:, :, gpsimd_from:CHUNK].rearrange("p j w -> p w j"),
+                    scalar1=1.0,
+                    scalar2=0.0,
+                    op0=MULT,
+                    op1=ADD,
                 )
             w_grouped[(c, g)] = grouped
 
@@ -147,18 +163,15 @@ def tile_attention_pa_kernel(tc, x, cos, sin, Wq, Wk, Wv, out_0, out_1, out_2):
                 in_=w_grouped[(c, g)][:].rearrange("p w j -> p (w j)"),
             )
 
-        def multiply(c):
-            banks = []
-            for t in range(S_TILES):
-                acc = psum.tile([P, CHUNK], F32, tag="bank")
-                banks.append(acc)
-            if c == len(chunks) - 1:
-                order = [(t, g) for g in range(PASSES) for t in range(S_TILES)]
-            else:
-                order = [(t, g) for t in range(S_TILES) for g in range(PASSES)]
+        banks = {}
+
+        def multiply(c, order):
             for t, g in order:
+                if (c, t) not in banks:
+                    acc = psum.tile([P, CHUNK], F32, tag="bank")
+                    banks[(c, t)] = acc
                 nc.tensor.matmul_mx(
-                    out=banks[t][:],
+                    out=banks[(c, t)][:],
                     lhsT=x_codes[t][:, g * P : (g + 1) * P].bitcast(FP8X4),
                     lhsT_scale=x_scales[t][:, g * P : (g + 1) * P],
                     rhs=w_codes[c][:, g, :].bitcast(FP8X4),
@@ -166,17 +179,24 @@ def tile_attention_pa_kernel(tc, x, cos, sin, Wq, Wk, Wv, out_0, out_1, out_2):
                     start=(g == 0),
                     stop=(g == PASSES - 1),
                 )
-            return banks
 
-        def rotate(acc, t, result):
-            straight = result[:, :, t, :]
+        results = {}
+        crosses = {}
+
+        def new_result(c):
+            result = result_pool.tile([P, HEADS, S_TILES, DH], F32)
+            results[c] = result
+
+        def multiply_straight(c, t):
             nc.vector.tensor_tensor(
-                out=straight,
-                in0=acc[:].rearrange("p (h d) -> p h d", h=HEADS),
+                out=results[c][:, :, t, :],
+                in0=banks[(c, t)][:].rearrange("p (h d) -> p h d", h=HEADS),
                 in1=cos_sb[:, t, :].unsqueeze(1).to_broadcast([P, HEADS, DH]),
                 op=MULT,
             )
-            swapped = acc[:].rearrange("p (h i e) -> p h i e", h=HEADS, e=2)[:, :, :, ::-1]
+
+        def multiply_cross(c, t):
+            swapped = banks[(c, t)][:].rearrange("p (h i e) -> p h i e", h=HEADS, e=2)[:, :, :, ::-1]
             cross = cross_pool.tile([P, HEADS, PAIRS, 2], F32)
             nc.vector.tensor_tensor(
                 out=cross[:],
@@ -184,45 +204,105 @@ def tile_attention_pa_kernel(tc, x, cos, sin, Wq, Wk, Wv, out_0, out_1, out_2):
                 in1=signed_sin[:, t, :, :].unsqueeze(1).to_broadcast([P, HEADS, PAIRS, 2]),
                 op=MULT,
             )
-            nc.vector.tensor_tensor(
+            crosses[(c, t)] = cross
+
+        def add(c, t, engine):
+            straight = results[c][:, :, t, :]
+            engine.tensor_tensor(
                 out=straight,
                 in0=straight,
-                in1=cross[:].rearrange("p h i e -> p h (i e)"),
+                in1=crosses[(c, t)][:].rearrange("p h i e -> p h (i e)"),
                 op=ADD,
             )
 
-        for g in range(PASSES):
-            if g == 2:
-                turn_x(0)
-            regroup(0, g)
-            quantise(0, g)
-        for t in range(1, S_TILES):
-            turn_x(t)
-        for c in range(1, AHEAD):
-            for g in range(PASSES):
-                regroup(c, g)
-                quantise(c, g)
-
-        def store(c, result, first_tile, end_tile):
+        def store(c, first_tile, end_tile):
             nc.sync.dma_start(
                 out=chunks[c][1][:, :, first_tile:end_tile, :].rearrange("p h t d -> p h (t d)"),
-                in_=result[:, :, first_tile:end_tile, :].rearrange("p h t d -> p h (t d)"),
+                in_=results[c][:, :, first_tile:end_tile, :].rearrange("p h t d -> p h (t d)"),
             )
 
-        last_rotated = max(c for c in range(len(chunks)) if chunks[c][2])
-        for c in range(len(chunks)):
-            banks = multiply(c)
-            result = result_pool.tile([P, HEADS, S_TILES, DH], F32)
+        def prepare(c, g):
+            quantise(c, g)
+            multiply(c, [(t, g) for t in range(S_TILES)])
+
+        last = len(chunks) - 1
+        engines = {
+            mybir.EngineType.PE,
+            mybir.EngineType.Activation,
+            mybir.EngineType.DVE,
+            mybir.EngineType.Pool,
+        }
+        with tc.manual_schedule(engines=engines):
+            new_result(0)
+            regroup(0, 0)
+            regroup(0, 1)
+            quantise(0, 0)
+            quantise(0, 1)
+            transpose_x(0)
+            copy_x(0)
+            regroup(0, 2)
+            quantise_x(0)
+            regroup(0, 3)
+            quantise(0, 2)
+            multiply(0, [(0, 0), (0, 1)])
+            transpose_x(1)
+            quantise(0, 3)
+            multiply(0, [(0, 2), (0, 3)])
+            copy_x(1)
+            transpose_x(2)
+            copy_x(2)
+            multiply_straight(0, 0)
+            quantise_x(1)
+            multiply_cross(0, 0)
+            multiply(0, [(1, g) for g in range(PASSES)])
+            regroup(1, 0)
+            transpose_x(3)
+            copy_x(3)
+            quantise_x(2)
+            add(0, 0, nc.vector)
+            multiply(0, [(2, g) for g in range(PASSES)])
+            multiply_straight(0, 1)
+            multiply_cross(0, 1)
+            regroup(1, 1)
+            quantise_x(3)
+            add(0, 1, nc.vector)
+            multiply(0, [(3, g) for g in range(PASSES)])
+            multiply_straight(0, 2)
+            multiply_cross(0, 2)
+            prepare(1, 0)
+            add(0, 2, nc.vector)
+            regroup(1, 2)
+            multiply_straight(0, 3)
+            multiply_cross(0, 3)
+            prepare(1, 1)
+            add(0, 3, nc.vector)
+            store(0, 0, S_TILES)
+            regroup(1, 3)
+            prepare(1, 2)
+            regroup(2, 0)
+            prepare(1, 3)
+            prepare(2, 0)
+
+            passes = [(c, g) for c in range(2, len(chunks)) for g in range(PASSES)]
+            done = 1
+            for c in range(1, last):
+                new_result(c)
+                for t in range(S_TILES):
+                    count = 1 if c < last - 1 else len(passes) - done
+                    ahead = passes[done : done + count]
+                    done += len(ahead)
+                    for n, g in ahead:
+                        regroup(n, g)
+                    multiply_straight(c, t)
+                    multiply_cross(c, t)
+                    for n, g in ahead:
+                        prepare(n, g)
+                    add(c, t, nc.vector)
+                    if c == last - 1:
+                        store(c, t, t + 1)
+                if c < last - 1:
+                    store(c, 0, S_TILES)
+            new_result(last)
             for t in range(S_TILES):
-                if c + AHEAD < len(chunks):
-                    regroup(c + AHEAD, t)
-                if chunks[c][2]:
-                    rotate(banks[t], t, result)
-                else:
-                    nc.scalar.copy(out=result[:, :, t, :], in_=banks[t][:].rearrange("p (h d) -> p h d", h=HEADS))
-                if c + AHEAD < len(chunks):
-                    quantise(c + AHEAD, t)
-                if c >= last_rotated:
-                    store(c, result, t, t + 1)
-            if c < last_rotated:
-                store(c, result, 0, S_TILES)
+                nc.scalar.copy(out=results[last][:, :, t, :], in_=banks[(last, t)][:].rearrange("p (h d) -> p h d", h=HEADS))
+                store(last, t, t + 1)

@@ -24,7 +24,7 @@ CHUNK = 512
 HEADS = CHUNK // DH
 AHEAD = 2
 VECTOR_COLS = (320, 64, 0, 0, 0, 0)
-GPSIMD_COLS = (0, 96, 96, 96, 96, 96)
+GPSIMD_COLS = (0, 96, 64, 64, 64, 64)
 
 FLOPS = 2 * S * D * (2048 + 512 + 512)
 
@@ -134,6 +134,7 @@ def tile_attention_pa_kernel(tc, x, cos, sin, Wq, Wk, Wv, out_0, out_1, out_2):
                 w_scales[c] = w_code_pool.tile([P, PASSES, CHUNK], U8, name="w_scales", align_bytes=64)
             raw = chunks[c][0][g]
             grouped = w_group_pool.tile([P, CHUNK, PACK], BF16, name="w_grouped", align_bytes=64)
+            w_grouped[(c, g)] = grouped
             gpsimd_from = CHUNK - GPSIMD_COLS[c]
             split = gpsimd_from - VECTOR_COLS[c]
             nc.scalar.copy(
@@ -145,6 +146,11 @@ def tile_attention_pa_kernel(tc, x, cos, sin, Wq, Wk, Wv, out_0, out_1, out_2):
                     out=grouped[:, split:gpsimd_from, :].rearrange("p (c i) j -> p c j i", i=4),
                     in_=raw[:, :, split:gpsimd_from].rearrange("p j (c i) -> p c j i", i=4),
                 )
+
+        def regroup_gpsimd(c, g):
+            raw = chunks[c][0][g]
+            grouped = w_grouped[(c, g)]
+            gpsimd_from = CHUNK - GPSIMD_COLS[c]
             if gpsimd_from < CHUNK:
                 nc.gpsimd.tensor_scalar(
                     out=grouped[:, gpsimd_from:CHUNK, :],
@@ -154,7 +160,6 @@ def tile_attention_pa_kernel(tc, x, cos, sin, Wq, Wk, Wv, out_0, out_1, out_2):
                     op0=MULT,
                     op1=ADD,
                 )
-            w_grouped[(c, g)] = grouped
 
         def quantise(c, g):
             nc.vector.quantize_mx(
@@ -256,6 +261,7 @@ def tile_attention_pa_kernel(tc, x, cos, sin, Wq, Wk, Wv, out_0, out_1, out_2):
             multiply_cross(0, 0)
             multiply(0, [(1, g) for g in range(PASSES)])
             regroup(1, 0)
+            regroup_gpsimd(1, 0)
             transpose_x(3)
             copy_x(3)
             quantise_x(2)
@@ -264,6 +270,7 @@ def tile_attention_pa_kernel(tc, x, cos, sin, Wq, Wk, Wv, out_0, out_1, out_2):
             multiply_straight(0, 1)
             multiply_cross(0, 1)
             regroup(1, 1)
+            regroup_gpsimd(1, 1)
             quantise_x(3)
             add(0, 1, nc.vector)
             multiply(0, [(3, g) for g in range(PASSES)])
@@ -272,36 +279,58 @@ def tile_attention_pa_kernel(tc, x, cos, sin, Wq, Wk, Wv, out_0, out_1, out_2):
             prepare(1, 0)
             add(0, 2, nc.vector)
             regroup(1, 2)
+            regroup_gpsimd(1, 2)
             multiply_straight(0, 3)
             multiply_cross(0, 3)
             prepare(1, 1)
             add(0, 3, nc.vector)
             store(0, 0, S_TILES)
             regroup(1, 3)
+            regroup_gpsimd(1, 3)
             prepare(1, 2)
-            regroup(2, 0)
+            for g in range(3):
+                regroup(2, g)
+                regroup_gpsimd(2, g)
             prepare(1, 3)
             prepare(2, 0)
+            regroup(2, 3)
+            regroup_gpsimd(2, 3)
+            regroup(3, 0)
+            regroup_gpsimd(3, 0)
 
             passes = [(c, g) for c in range(2, len(chunks)) for g in range(PASSES)]
             done = 1
+            left = []
             for c in range(1, last):
                 new_result(c)
-                for t in range(S_TILES):
-                    count = 1 if c < last - 1 else len(passes) - done
-                    ahead = passes[done : done + count]
-                    done += len(ahead)
-                    for n, g in ahead:
-                        regroup(n, g)
-                    multiply_straight(c, t)
-                    multiply_cross(c, t)
-                    for n, g in ahead:
+                for t in range(0, S_TILES, 2):
+                    for i in range(2):
+                        multiply_straight(c, t + i)
+                        multiply_cross(c, t + i)
+                    for n, i in left:
+                        add(n, i, nc.gpsimd)
+                        if i == S_TILES - 1:
+                            store(n, 0, S_TILES)
+                    left = []
+                    count = 2 if c < last - 1 else len(passes) - done
+                    for n, g in passes[done : done + count]:
                         prepare(n, g)
-                    add(c, t, nc.vector)
-                    if c == last - 1:
-                        store(c, t, t + 1)
-                if c < last - 1:
-                    store(c, 0, S_TILES)
+                    if c < last - 1:
+                        add(c, t, nc.vector)
+                        left.append((c, t + 1))
+                    elif t == 0:
+                        left.append((c, t))
+                    else:
+                        store(c, 0, 1)
+                        for i in range(1, S_TILES):
+                            add(c, i, nc.vector)
+                            store(c, i, i + 1)
+                    following = passes[done + 4 : done + 4 + count]
+                    done += count
+                    for n, g in following:
+                        regroup(n, g)
+                    for n, g in following[::-1]:
+                        regroup_gpsimd(n, g)
             new_result(last)
             for t in range(S_TILES):
                 nc.scalar.copy(out=results[last][:, :, t, :], in_=banks[(last, t)][:].rearrange("p (h d) -> p h d", h=HEADS))

@@ -24,7 +24,7 @@ CHUNK = 512
 HEADS = CHUNK // DH
 AHEAD = 2
 VECTOR_COLS = (320, 64, 0, 0, 0, 0)
-GPSIMD_COLS = (0, 96, 64, 64, 64, 64)
+GPSIMD_COLS = 96
 
 FLOPS = 2 * S * D * (2048 + 512 + 512)
 
@@ -128,6 +128,11 @@ def tile_attention_pa_kernel(tc, x, cos, sin, Wq, Wk, Wv, out_0, out_1, out_2):
         w_scales = {}
         w_grouped = {}
 
+        def gpsimd_start(c, g):
+            if c == 1 or (c > 1 and g % 2 == 0):
+                return CHUNK - GPSIMD_COLS
+            return CHUNK
+
         def regroup(c, g):
             if g == 0:
                 w_codes[c] = w_code_pool.tile([P, PASSES, CHUNK], U32, name="w_codes", align_bytes=64)
@@ -135,7 +140,7 @@ def tile_attention_pa_kernel(tc, x, cos, sin, Wq, Wk, Wv, out_0, out_1, out_2):
             raw = chunks[c][0][g]
             grouped = w_group_pool.tile([P, CHUNK, PACK], BF16, name="w_grouped", align_bytes=64)
             w_grouped[(c, g)] = grouped
-            gpsimd_from = CHUNK - GPSIMD_COLS[c]
+            gpsimd_from = gpsimd_start(c, g)
             split = gpsimd_from - VECTOR_COLS[c]
             nc.scalar.copy(
                 out=grouped[:, 0:split, :].rearrange("p (c i) j -> p c j i", i=4),
@@ -150,7 +155,7 @@ def tile_attention_pa_kernel(tc, x, cos, sin, Wq, Wk, Wv, out_0, out_1, out_2):
         def regroup_gpsimd(c, g):
             raw = chunks[c][0][g]
             grouped = w_grouped[(c, g)]
-            gpsimd_from = CHUNK - GPSIMD_COLS[c]
+            gpsimd_from = gpsimd_start(c, g)
             if gpsimd_from < CHUNK:
                 nc.gpsimd.tensor_scalar(
                     out=grouped[:, gpsimd_from:CHUNK, :],
@@ -309,22 +314,23 @@ def tile_attention_pa_kernel(tc, x, cos, sin, Wq, Wk, Wv, out_0, out_1, out_2):
                         multiply_cross(c, t + i)
                     for n, i in left:
                         add(n, i, nc.gpsimd)
-                        if i == S_TILES - 1:
+                        if n == last - 1:
+                            store(n, i, i + 1)
+                        elif i == S_TILES - 1:
                             store(n, 0, S_TILES)
                     left = []
-                    count = 2 if c < last - 1 else len(passes) - done
+                    count = 3 if (c, t) == (last - 2, 2) else 2
                     for n, g in passes[done : done + count]:
                         prepare(n, g)
-                    if c < last - 1:
-                        add(c, t, nc.vector)
-                        left.append((c, t + 1))
-                    elif t == 0:
-                        left.append((c, t))
+                    add(c, t, nc.vector)
+                    if (c, t) == (last - 1, 2):
+                        add(c, t + 1, nc.vector)
                     else:
-                        store(c, 0, 1)
-                        for i in range(1, S_TILES):
-                            add(c, i, nc.vector)
-                            store(c, i, i + 1)
+                        left.append((c, t + 1))
+                    if c == last - 1:
+                        store(c, t, t + 1)
+                    if (c, t) == (last - 1, 2):
+                        store(c, t + 1, t + 2)
                     following = passes[done + 4 : done + 4 + count]
                     done += count
                     for n, g in following:

@@ -143,8 +143,8 @@ def tile_attention_pa_kernel(tc, x, cos, sin, Wq, Wk, Wv, out_0, out_1, out_2):
             gpsimd_from = gpsimd_start(c, g)
             split = gpsimd_from - VECTOR_COLS[c]
             nc.scalar.copy(
-                out=grouped[:, 0:split, :].rearrange("p (c i) j -> p c j i", i=4),
-                in_=raw[:, :, 0:split].rearrange("p j (c i) -> p c j i", i=4),
+                out=grouped[:, 0:split, :].rearrange("p (c i) j -> p c j i", i=8),
+                in_=raw[:, :, 0:split].rearrange("p j (c i) -> p c j i", i=8),
             )
             if split < gpsimd_from:
                 nc.vector.tensor_copy(

@@ -23,8 +23,9 @@ PASSES = D // K_PASS
 CHUNK = 512
 HEADS = CHUNK // DH
 AHEAD = 2
-VECTOR_COLS = (320, 64, 0, 0, 0, 0)
-GPSIMD_COLS = 96
+VECTOR_COLS = (320, 0, 0, 0, 0, 0)
+PLACES = 4
+GPSIMD_COLS = 128
 
 FLOPS = 2 * S * D * (2048 + 512 + 512)
 
@@ -35,7 +36,7 @@ def tile_attention_pa_kernel(tc, x, cos, sin, Wq, Wk, Wv, out_0, out_1, out_2):
         consts = ctx.enter_context(tc.tile_pool(name="consts", bufs=1))
         raw_pool = ctx.enter_context(tc.tile_pool(name="raw", bufs=1))
         x_group_pool = ctx.enter_context(tc.tile_pool(name="x_group", bufs=2))
-        w_group_pool = ctx.enter_context(tc.tile_pool(name="w_group", bufs=4))
+        w_group_pool = ctx.enter_context(tc.tile_pool(name="w_group", bufs=PLACES))
         w_code_pool = ctx.enter_context(tc.tile_pool(name="w_code", bufs=AHEAD + 1))
         cross_pool = ctx.enter_context(tc.tile_pool(name="cross", bufs=4))
         result_pool = ctx.enter_context(tc.tile_pool(name="result", bufs=3))
@@ -74,16 +75,16 @@ def tile_attention_pa_kernel(tc, x, cos, sin, Wq, Wk, Wv, out_0, out_1, out_2):
         sin_sb = consts.tile([P, S_TILES, DH], BF16)
         nc.sync.dma_start(out=sin_sb[:].rearrange("p t d -> p (t d)"), in_=sin.rearrange("(p t) d -> p (t d)", t=S_TILES))
         nc.sync.dma_start(out=cos_sb[:].rearrange("p t d -> p (t d)"), in_=cos.rearrange("(p t) d -> p (t d)", t=S_TILES))
+        wq_tiles = load_passes(Wq, 0, "wq0", range(0, 1))
         for t in range(1, S_TILES):
             load_x(t)
-        for n in range(2048 // CHUNK):
+        wq_tiles.extend(load_passes(Wq, 0, "wq0", range(1, PASSES)))
+        chunks.append((wq_tiles, q_out[:, 0:HEADS, :, :], True))
+        for n in range(1, 2048 // CHUNK):
             chunks.append((load_chunk(Wq, n * CHUNK, "wq%d" % n), q_out[:, n * HEADS : (n + 1) * HEADS, :, :], True))
         chunks.append((load_chunk(Wv, 0, "wv"), v_out, False))
 
         sin_pairs = sin_sb[:].rearrange("p t (i e) -> p t i e", e=2)
-        signed_sin = consts.tile([P, S_TILES, PAIRS, 2], F32)
-        nc.gpsimd.tensor_scalar(out=signed_sin[:, :, :, 0], in0=sin_pairs[:, :, :, 0], scalar1=-1.0, scalar2=0.0, op0=MULT, op1=ADD)
-        nc.gpsimd.tensor_scalar(out=signed_sin[:, :, :, 1], in0=sin_pairs[:, :, :, 1], scalar1=1.0, scalar2=0.0, op0=MULT, op1=ADD)
 
         ident = consts.tile([P, P], F32)
         make_identity(nc, ident[:])
@@ -103,12 +104,12 @@ def tile_attention_pa_kernel(tc, x, cos, sin, Wq, Wk, Wv, out_0, out_1, out_2):
                     for u in range(2):
                         nc.tensor.transpose(turned[:, g2, u, :], words[:, 2 * half + g2, u, :], ident[:])
 
-        def copy_x(t):
+        def copy_x(t, engines):
             grouped_x = x_group_pool.tile([P, PASSES, P, PACK], BF16, align_bytes=64)
             x_grouped[t] = grouped_x
             grouped_words = grouped_x[:].bitcast(F32)
             for half in range(2):
-                nc.scalar.copy(
+                engines[half](
                     out=grouped_words[:, 2 * half : 2 * half + 2, :, :],
                     in_=x_banks[t][half][:].rearrange("p g u s -> p g s u"),
                 )
@@ -129,7 +130,7 @@ def tile_attention_pa_kernel(tc, x, cos, sin, Wq, Wk, Wv, out_0, out_1, out_2):
         w_grouped = {}
 
         def gpsimd_start(c, g):
-            if c == 1 or (c > 1 and g % 2 == 0):
+            if (c == 1 and g >= 2) or (c == 2 and g in (0, 3)) or (c >= 3 and g % 2 == 0):
                 return CHUNK - GPSIMD_COLS
             return CHUNK
 
@@ -211,7 +212,7 @@ def tile_attention_pa_kernel(tc, x, cos, sin, Wq, Wk, Wv, out_0, out_1, out_2):
             nc.vector.tensor_tensor(
                 out=cross[:],
                 in0=swapped,
-                in1=signed_sin[:, t, :, :].unsqueeze(1).to_broadcast([P, HEADS, PAIRS, 2]),
+                in1=sin_pairs[:, t, :, :].unsqueeze(1).to_broadcast([P, HEADS, PAIRS, 2]),
                 op=MULT,
             )
             crosses[(c, t)] = cross
@@ -235,6 +236,10 @@ def tile_attention_pa_kernel(tc, x, cos, sin, Wq, Wk, Wv, out_0, out_1, out_2):
             quantise(c, g)
             multiply(c, [(t, g) for t in range(S_TILES)])
 
+        def gpsimd_waits(written, dtype):
+            probe = cross_pool.tile([P, 1], dtype)
+            nc.gpsimd.tensor_copy(out=probe[:], in_=written)
+
         last = len(chunks) - 1
         engines = {
             mybir.EngineType.PE,
@@ -243,65 +248,73 @@ def tile_attention_pa_kernel(tc, x, cos, sin, Wq, Wk, Wv, out_0, out_1, out_2):
             mybir.EngineType.Pool,
         }
         with tc.manual_schedule(engines=engines):
+            both_scalar = (nc.scalar.copy, nc.scalar.copy)
             new_result(0)
             regroup(0, 0)
             regroup(0, 1)
             quantise(0, 0)
             quantise(0, 1)
             transpose_x(0)
-            copy_x(0)
+            copy_x(0, both_scalar)
             regroup(0, 2)
             quantise_x(0)
             regroup(0, 3)
             quantise(0, 2)
             multiply(0, [(0, 0), (0, 1)])
+            regroup(1, 0)
+            multiply(0, [(0, 2)])
             transpose_x(1)
             quantise(0, 3)
-            multiply(0, [(0, 2), (0, 3)])
-            copy_x(1)
+            nc.vector.tensor_scalar(out=sin_pairs[:, :, :, 0], in0=sin_pairs[:, :, :, 0], scalar1=-1.0, scalar2=None, op0=MULT)
+            multiply(0, [(0, 3)])
+            copy_x(1, (nc.scalar.copy, nc.vector.tensor_copy))
             transpose_x(2)
-            copy_x(2)
+            copy_x(2, both_scalar)
+            transpose_x(3)
+            copy_x(3, both_scalar)
             multiply_straight(0, 0)
             quantise_x(1)
             multiply_cross(0, 0)
             multiply(0, [(1, g) for g in range(PASSES)])
-            regroup(1, 0)
-            regroup_gpsimd(1, 0)
-            transpose_x(3)
-            copy_x(3)
             quantise_x(2)
             add(0, 0, nc.vector)
+            gpsimd_waits(results[0][:, 0, 0, 0:1], F32)
             multiply(0, [(2, g) for g in range(PASSES)])
-            multiply_straight(0, 1)
-            multiply_cross(0, 1)
             regroup(1, 1)
-            regroup_gpsimd(1, 1)
-            quantise_x(3)
-            add(0, 1, nc.vector)
-            multiply(0, [(3, g) for g in range(PASSES)])
-            multiply_straight(0, 2)
-            multiply_cross(0, 2)
-            prepare(1, 0)
-            add(0, 2, nc.vector)
             regroup(1, 2)
             regroup_gpsimd(1, 2)
-            multiply_straight(0, 3)
-            multiply_cross(0, 3)
-            prepare(1, 1)
-            add(0, 3, nc.vector)
-            store(0, 0, S_TILES)
+            multiply_straight(0, 1)
+            multiply_cross(0, 1)
+            quantise_x(3)
+            add(0, 1, nc.vector)
+            gpsimd_waits(results[0][:, 0, 1, 0:1], F32)
+            multiply(0, [(3, g) for g in range(PASSES)])
             regroup(1, 3)
             regroup_gpsimd(1, 3)
-            prepare(1, 2)
-            for g in range(3):
-                regroup(2, g)
-                regroup_gpsimd(2, g)
-            prepare(1, 3)
-            prepare(2, 0)
+            multiply_straight(0, 2)
+            multiply_cross(0, 2)
+            quantise(1, 0)
+            quantise(1, 1)
+            multiply(1, [(t, g) for g in range(2) for t in range(S_TILES)])
+            add(0, 2, nc.vector)
+            gpsimd_waits(results[0][:, 0, 2, 0:1], F32)
+            regroup(2, 0)
+            regroup_gpsimd(2, 0)
+            regroup(2, 1)
+            multiply_straight(0, 3)
+            multiply_cross(0, 3)
+            quantise(1, 2)
+            quantise(1, 3)
+            for first in range(0, S_TILES, 2):
+                multiply(1, [(t, g) for g in range(2, PASSES) for t in range(first, first + 2)])
+            regroup(2, 2)
             regroup(2, 3)
-            regroup_gpsimd(2, 3)
+            prepare(2, 0)
+            add(0, 3, nc.vector)
+            store(0, 0, S_TILES)
             regroup(3, 0)
             regroup_gpsimd(3, 0)
+            regroup_gpsimd(2, 3)
 
             passes = [(c, g) for c in range(2, len(chunks)) for g in range(PASSES)]
             done = 1
@@ -319,7 +332,7 @@ def tile_attention_pa_kernel(tc, x, cos, sin, Wq, Wk, Wv, out_0, out_1, out_2):
                         elif i == S_TILES - 1:
                             store(n, 0, S_TILES)
                     left = []
-                    count = 3 if (c, t) == (last - 2, 2) else 2
+                    count = 2 if c < last - 1 else len(passes) - done
                     for n, g in passes[done : done + count]:
                         prepare(n, g)
                     add(c, t, nc.vector)
@@ -331,12 +344,15 @@ def tile_attention_pa_kernel(tc, x, cos, sin, Wq, Wk, Wv, out_0, out_1, out_2):
                         store(c, t, t + 1)
                     if (c, t) == (last - 1, 2):
                         store(c, t + 1, t + 2)
-                    following = passes[done + 4 : done + 4 + count]
+                    following = passes[done + PLACES : done + PLACES + count]
                     done += count
                     for n, g in following:
                         regroup(n, g)
                     for n, g in following[::-1]:
                         regroup_gpsimd(n, g)
+                    if all(gpsimd_start(n, g) == CHUNK for n, g in following):
+                        n, g = passes[min(done, len(passes)) - 1]
+                        gpsimd_waits(w_codes[n][:, g, 0:1], U32)
             new_result(last)
             for t in range(S_TILES):
                 nc.scalar.copy(out=results[last][:, :, t, :], in_=banks[(last, t)][:].rearrange("p (h d) -> p h d", h=HEADS))

@@ -39,7 +39,7 @@ def tile_attention_pa_kernel(tc, x, cos, sin, Wq, Wk, Wv, out_0, out_1, out_2):
         w_group_pool = ctx.enter_context(tc.tile_pool(name="w_group", bufs=PLACES))
         w_code_pool = ctx.enter_context(tc.tile_pool(name="w_code", bufs=AHEAD + 1))
         cross_pool = ctx.enter_context(tc.tile_pool(name="cross", bufs=4))
-        result_pool = ctx.enter_context(tc.tile_pool(name="result", bufs=3))
+        result_pool = ctx.enter_context(tc.tile_pool(name="result", bufs=5))
         psum = ctx.enter_context(tc.psum_pool(name="psum", bufs=8))
 
         def load_passes(w, first_col, label, passes):
@@ -356,4 +356,4 @@ def tile_attention_pa_kernel(tc, x, cos, sin, Wq, Wk, Wv, out_0, out_1, out_2):
             new_result(last)
             for t in range(S_TILES):
                 nc.scalar.copy(out=results[last][:, :, t, :], in_=banks[(last, t)][:].rearrange("p (h d) -> p h d", h=HEADS))
-                store(last, t, t + 1)
+            store(last, 0, S_TILES)

from contextlib import ExitStack

import concourse.mybir as mybir
from concourse.masks import make_identity

F32 = mybir.dt.float32
BF16 = mybir.dt.bfloat16
U32 = mybir.dt.uint32
U8 = mybir.dt.uint8
FP8X4 = mybir.dt.float8_e4m3fn_x4
MULT = mybir.AluOpType.mult
ADD = mybir.AluOpType.add

P = 128
PACK = 4
K_PASS = P * PACK
S = 512
D = 2048
DH = 128
PAIRS = DH // 2
S_TILES = S // P
PASSES = D // K_PASS
CHUNK = 512
HEADS = CHUNK // DH
AHEAD = 2
VECTOR_COLS = (320, 0, 0, 0, 0, 0)
PLACES = 4
GPSIMD_COLS = 128

FLOPS = 2 * S * D * (2048 + 512 + 512)


def tile_attention_pa_kernel(tc, x, cos, sin, Wq, Wk, Wv, out_0, out_1, out_2):
    nc = tc.nc
    with ExitStack() as ctx:
        consts = ctx.enter_context(tc.tile_pool(name="consts", bufs=1))
        raw_pool = ctx.enter_context(tc.tile_pool(name="raw", bufs=1))
        x_group_pool = ctx.enter_context(tc.tile_pool(name="x_group", bufs=2))
        w_group_pool = ctx.enter_context(tc.tile_pool(name="w_group", bufs=PLACES))
        w_code_pool = ctx.enter_context(tc.tile_pool(name="w_code", bufs=AHEAD + 1))
        cross_pool = ctx.enter_context(tc.tile_pool(name="cross", bufs=4))
        result_pool = ctx.enter_context(tc.tile_pool(name="result", bufs=5))
        psum = ctx.enter_context(tc.psum_pool(name="psum", bufs=8))

        def load_passes(w, first_col, label, passes):
            by_pass = w.rearrange("(g p j) n -> g p j n", p=P, j=PACK)
            tiles = []
            for g in passes:
                raw = raw_pool.tile([P, PACK, CHUNK], BF16, name="%s_pass%d" % (label, g))
                nc.sync.dma_start(out=raw[:], in_=by_pass[g, :, :, first_col : first_col + CHUNK])
                tiles.append(raw)
            return tiles

        def load_chunk(w, first_col, label):
            return load_passes(w, first_col, label, range(PASSES))

        q_out = out_0.rearrange("b h (p t) d -> p (b h) t d", t=S_TILES)
        k_out = out_1.rearrange("b h (p t) d -> p (b h) t d", t=S_TILES)
        v_out = out_2.rearrange("b h (p t) d -> p (b h) t d", t=S_TILES)

        chunks = []
        x_rows = x.rearrange("b (p t) k -> t p (b k)", t=S_TILES)
        x_sb = []

        def load_x(t):
            x_t = raw_pool.tile([P, D], BF16, name="x_rows_%d" % t)
            nc.sync.dma_start(out=x_t[:], in_=x_rows[t])
            x_sb.append(x_t)

        wk_tiles = load_passes(Wk, 0, "wk", range(0, 2))
        load_x(0)
        wk_tiles.extend(load_passes(Wk, 0, "wk", range(2, PASSES)))
        chunks.append((wk_tiles, k_out, True))
        cos_sb = consts.tile([P, S_TILES, DH], BF16)
        sin_sb = consts.tile([P, S_TILES, DH], BF16)
        nc.sync.dma_start(out=sin_sb[:].rearrange("p t d -> p (t d)"), in_=sin.rearrange("(p t) d -> p (t d)", t=S_TILES))
        nc.sync.dma_start(out=cos_sb[:].rearrange("p t d -> p (t d)"), in_=cos.rearrange("(p t) d -> p (t d)", t=S_TILES))
        wq_tiles = load_passes(Wq, 0, "wq0", range(0, 1))
        for t in range(1, S_TILES):
            load_x(t)
        wq_tiles.extend(load_passes(Wq, 0, "wq0", range(1, PASSES)))
        chunks.append((wq_tiles, q_out[:, 0:HEADS, :, :], True))
        for n in range(1, 2048 // CHUNK):
            chunks.append((load_chunk(Wq, n * CHUNK, "wq%d" % n), q_out[:, n * HEADS : (n + 1) * HEADS, :, :], True))
        chunks.append((load_chunk(Wv, 0, "wv"), v_out, False))

        sin_pairs = sin_sb[:].rearrange("p t (i e) -> p t i e", e=2)

        ident = consts.tile([P, P], F32)
        make_identity(nc, ident[:])
        x_codes = []
        x_scales = []

        x_banks = {}
        x_grouped = {}

        def transpose_x(t):
            words = x_sb[t][:].bitcast(F32).rearrange("s (g w u) -> s g u w", g=PASSES, u=2)
            x_banks[t] = []
            for half in range(2):
                turned = psum.tile([P, 2, 2, P], F32, tag="bank")
                x_banks[t].append(turned)
                for g2 in range(2):
                    for u in range(2):
                        nc.tensor.transpose(turned[:, g2, u, :], words[:, 2 * half + g2, u, :], ident[:])

        def copy_x(t, engines):
            grouped_x = x_group_pool.tile([P, PASSES, P, PACK], BF16, align_bytes=64)
            x_grouped[t] = grouped_x
            grouped_words = grouped_x[:].bitcast(F32)
            for half in range(2):
                engines[half](
                    out=grouped_words[:, 2 * half : 2 * half + 2, :, :],
                    in_=x_banks[t][half][:].rearrange("p g u s -> p g s u"),
                )

        def quantise_x(t):
            codes_t = consts.tile([P, PASSES * P], U32, name="x_codes_%d" % t, align_bytes=64)
            scales_t = consts.tile([P, PASSES * P], U8, name="x_scales_%d" % t, align_bytes=64)
            nc.vector.quantize_mx(
                out=codes_t[:].bitcast(FP8X4),
                scales=scales_t[:],
                in_=x_grouped[t][:].rearrange("p g s j -> p (g s j)"),
            )
            x_codes.append(codes_t)
            x_scales.append(scales_t)

        w_codes = {}
        w_scales = {}
        w_grouped = {}

        def gpsimd_start(c, g):
            if (c == 1 and g >= 2) or (c == 2 and g in (0, 3)) or (c >= 3 and g % 2 == 0):
                return CHUNK - GPSIMD_COLS
            return CHUNK

        def regroup(c, g):
            if g == 0:
                w_codes[c] = w_code_pool.tile([P, PASSES, CHUNK], U32, name="w_codes", align_bytes=64)
                w_scales[c] = w_code_pool.tile([P, PASSES, CHUNK], U8, name="w_scales", align_bytes=64)
            raw = chunks[c][0][g]
            grouped = w_group_pool.tile([P, CHUNK, PACK], BF16, name="w_grouped", align_bytes=64)
            w_grouped[(c, g)] = grouped
            gpsimd_from = gpsimd_start(c, g)
            split = gpsimd_from - VECTOR_COLS[c]
            nc.scalar.copy(
                out=grouped[:, 0:split, :].rearrange("p (c i) j -> p c j i", i=8),
                in_=raw[:, :, 0:split].rearrange("p j (c i) -> p c j i", i=8),
            )
            if split < gpsimd_from:
                nc.vector.tensor_copy(
                    out=grouped[:, split:gpsimd_from, :].rearrange("p (c i) j -> p c j i", i=4),
                    in_=raw[:, :, split:gpsimd_from].rearrange("p j (c i) -> p c j i", i=4),
                )

        def regroup_gpsimd(c, g):
            raw = chunks[c][0][g]
            grouped = w_grouped[(c, g)]
            gpsimd_from = gpsimd_start(c, g)
            if gpsimd_from < CHUNK:
                nc.gpsimd.tensor_scalar(
                    out=grouped[:, gpsimd_from:CHUNK, :],
                    in0=raw[:, :, gpsimd_from:CHUNK].rearrange("p j w -> p w j"),
                    scalar1=1.0,
                    scalar2=0.0,
                    op0=MULT,
                    op1=ADD,
                )

        def quantise(c, g):
            nc.vector.quantize_mx(
                out=w_codes[c][:, g, :].bitcast(FP8X4),
                scales=w_scales[c][:, g, :],
                in_=w_grouped[(c, g)][:].rearrange("p w j -> p (w j)"),
            )

        banks = {}

        def multiply(c, order):
            for t, g in order:
                if (c, t) not in banks:
                    acc = psum.tile([P, CHUNK], F32, tag="bank")
                    banks[(c, t)] = acc
                nc.tensor.matmul_mx(
                    out=banks[(c, t)][:],
                    lhsT=x_codes[t][:, g * P : (g + 1) * P].bitcast(FP8X4),
                    lhsT_scale=x_scales[t][:, g * P : (g + 1) * P],
                    rhs=w_codes[c][:, g, :].bitcast(FP8X4),
                    rhs_scale=w_scales[c][:, g, :],
                    start=(g == 0),
                    stop=(g == PASSES - 1),
                )

        results = {}
        crosses = {}

        def new_result(c):
            result = result_pool.tile([P, HEADS, S_TILES, DH], F32)
            results[c] = result

        def multiply_straight(c, t):
            nc.vector.tensor_tensor(
                out=results[c][:, :, t, :],
                in0=banks[(c, t)][:].rearrange("p (h d) -> p h d", h=HEADS),
                in1=cos_sb[:, t, :].unsqueeze(1).to_broadcast([P, HEADS, DH]),
                op=MULT,
            )

        def multiply_cross(c, t):
            swapped = banks[(c, t)][:].rearrange("p (h i e) -> p h i e", h=HEADS, e=2)[:, :, :, ::-1]
            cross = cross_pool.tile([P, HEADS, PAIRS, 2], F32)
            nc.vector.tensor_tensor(
                out=cross[:],
                in0=swapped,
                in1=sin_pairs[:, t, :, :].unsqueeze(1).to_broadcast([P, HEADS, PAIRS, 2]),
                op=MULT,
            )
            crosses[(c, t)] = cross

        def add(c, t, engine):
            straight = results[c][:, :, t, :]
            engine.tensor_tensor(
                out=straight,
                in0=straight,
                in1=crosses[(c, t)][:].rearrange("p h i e -> p h (i e)"),
                op=ADD,
            )

        def store(c, first_tile, end_tile):
            nc.sync.dma_start(
                out=chunks[c][1][:, :, first_tile:end_tile, :].rearrange("p h t d -> p h (t d)"),
                in_=results[c][:, :, first_tile:end_tile, :].rearrange("p h t d -> p h (t d)"),
            )

        def prepare(c, g):
            quantise(c, g)
            multiply(c, [(t, g) for t in range(S_TILES)])

        def gpsimd_waits(written, dtype):
            probe = cross_pool.tile([P, 1], dtype)
            nc.gpsimd.tensor_copy(out=probe[:], in_=written)

        last = len(chunks) - 1
        engines = {
            mybir.EngineType.PE,
            mybir.EngineType.Activation,
            mybir.EngineType.DVE,
            mybir.EngineType.Pool,
        }
        with tc.manual_schedule(engines=engines):
            both_scalar = (nc.scalar.copy, nc.scalar.copy)
            new_result(0)
            regroup(0, 0)
            regroup(0, 1)
            quantise(0, 0)
            quantise(0, 1)
            transpose_x(0)
            copy_x(0, both_scalar)
            regroup(0, 2)
            quantise_x(0)
            regroup(0, 3)
            quantise(0, 2)
            multiply(0, [(0, 0), (0, 1)])
            regroup(1, 0)
            multiply(0, [(0, 2)])
            transpose_x(1)
            quantise(0, 3)
            nc.vector.tensor_scalar(out=sin_pairs[:, :, :, 0], in0=sin_pairs[:, :, :, 0], scalar1=-1.0, scalar2=None, op0=MULT)
            multiply(0, [(0, 3)])
            copy_x(1, (nc.scalar.copy, nc.vector.tensor_copy))
            transpose_x(2)
            copy_x(2, both_scalar)
            transpose_x(3)
            copy_x(3, both_scalar)
            multiply_straight(0, 0)
            quantise_x(1)
            multiply_cross(0, 0)
            multiply(0, [(1, g) for g in range(PASSES)])
            quantise_x(2)
            add(0, 0, nc.vector)
            gpsimd_waits(results[0][:, 0, 0, 0:1], F32)
            multiply(0, [(2, g) for g in range(PASSES)])
            regroup(1, 1)
            regroup(1, 2)
            regroup_gpsimd(1, 2)
            multiply_straight(0, 1)
            multiply_cross(0, 1)
            quantise_x(3)
            add(0, 1, nc.vector)
            gpsimd_waits(results[0][:, 0, 1, 0:1], F32)
            multiply(0, [(3, g) for g in range(PASSES)])
            regroup(1, 3)
            regroup_gpsimd(1, 3)
            multiply_straight(0, 2)
            multiply_cross(0, 2)
            quantise(1, 0)
            quantise(1, 1)
            multiply(1, [(t, g) for g in range(2) for t in range(S_TILES)])
            add(0, 2, nc.vector)
            gpsimd_waits(results[0][:, 0, 2, 0:1], F32)
            regroup(2, 0)
            regroup_gpsimd(2, 0)
            regroup(2, 1)
            multiply_straight(0, 3)
            multiply_cross(0, 3)
            quantise(1, 2)
            quantise(1, 3)
            for first in range(0, S_TILES, 2):
                multiply(1, [(t, g) for g in range(2, PASSES) for t in range(first, first + 2)])
            regroup(2, 2)
            regroup(2, 3)
            prepare(2, 0)
            add(0, 3, nc.vector)
            store(0, 0, S_TILES)
            regroup(3, 0)
            regroup_gpsimd(3, 0)
            regroup_gpsimd(2, 3)

            passes = [(c, g) for c in range(2, len(chunks)) for g in range(PASSES)]
            done = 1
            left = []
            for c in range(1, last):
                new_result(c)
                for t in range(0, S_TILES, 2):
                    for i in range(2):
                        multiply_straight(c, t + i)
                        multiply_cross(c, t + i)
                    for n, i in left:
                        add(n, i, nc.gpsimd)
                        if n == last - 1:
                            store(n, i, i + 1)
                        elif i == S_TILES - 1:
                            store(n, 0, S_TILES)
                    left = []
                    count = 2 if c < last - 1 else len(passes) - done
                    for n, g in passes[done : done + count]:
                        prepare(n, g)
                    add(c, t, nc.vector)
                    if (c, t) == (last - 1, 2):
                        add(c, t + 1, nc.vector)
                    else:
                        left.append((c, t + 1))
                    if c == last - 1:
                        store(c, t, t + 1)
                    if (c, t) == (last - 1, 2):
                        store(c, t + 1, t + 2)
                    following = passes[done + PLACES : done + PLACES + count]
                    done += count
                    for n, g in following:
                        regroup(n, g)
                    for n, g in following[::-1]:
                        regroup_gpsimd(n, g)
                    if all(gpsimd_start(n, g) == CHUNK for n, g in following):
                        n, g = passes[min(done, len(passes)) - 1]
                        gpsimd_waits(w_codes[n][:, g, 0:1], U32)
            new_result(last)
            for t in range(S_TILES):
                nc.scalar.copy(out=results[last][:, :, t, :], in_=banks[(last, t)][:].rearrange("p (h d) -> p h d", h=HEADS))
            store(last, 0, S_TILES)
